import numpy as np
import ml_dtypes


def mxq(x, axis, fmt="e4m3"):
    dtype, down = {"e4m3": (ml_dtypes.float8_e4m3fn, 7), "e5m2": (ml_dtypes.float8_e5m2, 14)}[fmt]
    v = np.moveaxis(np.asarray(x, np.float32).astype(ml_dtypes.bfloat16).astype(np.float64), axis, -1)
    blocks = v.reshape(v.shape[:-1] + (-1, 32))
    amax = np.abs(blocks).max(-1, keepdims=True)
    byte = np.maximum(np.where(amax > 0, np.frexp(amax)[1] - 1 + 127, 0) - down, 1)
    scale = np.exp2(byte - 127.0)
    codes = (blocks / scale).astype(np.float32).astype(dtype).astype(np.float64)
    return np.moveaxis((codes * scale).reshape(v.shape), -1, axis)


WIDE = False


def mx_kscale(k):
    if not WIDE:
        return np.ones(k)
    levels = np.array([10, -10, 5, -5, 0])
    a = np.random.permutation(np.resize(levels, k // 512 * 4)).reshape(k // 512, 4)
    idx = np.arange(k)
    return np.exp2(a[idx // 512, idx % 128 // 32])


BF16 = ml_dtypes.bfloat16


def bf(x):
    return np.asarray(x, np.float32).astype(BF16)


def f64(x):
    return np.asarray(x).astype(np.float64)


B, L, D, DK = 8, 512, 512, 128


def setup_inputs():
    s = mx_kscale(D)
    z = np.random.standard_normal((B, L, L)) * 2.0
    e = np.exp(z - z.max(-1, keepdims=True))
    return {"x": bf(np.random.standard_normal((B, L, D)) * s),
            "Wv1": bf(np.random.standard_normal((D, D)) * 2.0 / np.sqrt(D) / s),
            "bv1": bf(np.random.standard_normal(D) * 0.5),
            "att2": bf(e / e.sum(-1, keepdims=True)),
            "gamma2": bf(1.0 + 0.1 * np.random.standard_normal(1)),
            "y": bf(np.random.standard_normal((B, L, D)))}


def reference(x, Wv1, bv1, att2, gamma2, y):
    v1 = (mxq(f64(x), 2, "e4m3") @ mxq(f64(Wv1).T, 0, "e4m3")) + f64(bv1)
    o = mxq(v1.transpose(0, 2, 1), 2, "e4m3") @ mxq(f64(att2), 1, "e4m3")
    return f64(gamma2) * o.reshape(B, L, D) + f64(y)

@@ -1,0 +1,171 @@
+from contextlib import ExitStack
+
+import concourse.mybir as mybir
+from concourse.masks import make_identity
+
+BF16 = mybir.dt.bfloat16
+F32 = mybir.dt.float32
+U32 = mybir.dt.uint32
+U8 = mybir.dt.uint8
+FP8X4 = mybir.dt.float8_e4m3fn_x4
+ADD = mybir.AluOpType.add
+MULT = mybir.AluOpType.mult
+
+B = 8
+N = 512
+P = 128
+PACK = 4
+PAIR = 2
+GAMMA_COLS = 64
+
+FLOPS = 2 * B * (N * N * N + N * N * N)
+
+
+def tile_dualcrossmodalattention_pb_t_kernel(tc, x, Wv1, bv1, att2, gamma2, y, out):
+    nc = tc.nc
+    with ExitStack() as ctx:
+        const = ctx.enter_context(tc.tile_pool(name="const", bufs=1))
+        inputs = ctx.enter_context(tc.tile_pool(name="inputs", bufs=B))
+        grouped = ctx.enter_context(tc.tile_pool(name="grouped", bufs=2))
+        quantised = ctx.enter_context(tc.tile_pool(name="quantised", bufs=3))
+        results = ctx.enter_context(tc.tile_pool(name="results", bufs=3))
+        flip_psum = ctx.enter_context(tc.psum_pool(name="flip_psum", bufs=2))
+        v_psum = ctx.enter_context(tc.psum_pool(name="v_psum", bufs=3))
+        o_psum = ctx.enter_context(tc.psum_pool(name="o_psum", bufs=3))
+
+        def load_rows(matrix, name):
+            rows_sb = inputs.tile([P, PACK * N], BF16, tag=name, name=name)
+            nc.sync.dma_start(out=rows_sb[:], in_=matrix.rearrange("(p j) c -> p (j c)", j=PACK))
+            return rows_sb
+
+        small = const.tile([P, N + GAMMA_COLS], BF16)
+        nc.vector.memset(small[:], 0.0)
+        nc.sync.dma_start(out=small[0:1, 0:N], in_=bv1.rearrange("(o d) -> o d", o=1))
+        nc.sync.dma_start(out=small[0:1, N : N + 1], in_=gamma2.rearrange("(o g) -> o g", o=1))
+        w_sb = const.tile([P, PACK * N], BF16)
+        nc.sync.dma_start(out=w_sb[:], in_=Wv1.rearrange("(p j) c -> p (j c)", j=PACK))
+        x_in, att_in, y_in = [], [], []
+        for b in range(B):
+            x_in.append(load_rows(x[b], "x_sb"))
+            att_in.append(load_rows(att2[b], "att_sb"))
+            y_in.append(load_rows(y[b], "y_sb"))
+
+        ident = const.tile([P, P], F32)
+        make_identity(nc, ident[:])
+        ones = const.tile([P, P], BF16)
+        nc.vector.memset(ones[:], 1.0)
+
+        bias_ps = flip_psum.tile([P, N], F32, tag="flip")
+        nc.tensor.matmul(out=bias_ps[:], lhsT=ones[:], rhs=small[:, 0:N], start=True, stop=True)
+        gamma_ps = flip_psum.tile([P, GAMMA_COLS], F32, tag="flip")
+        nc.tensor.matmul(out=gamma_ps[:], lhsT=ones[:], rhs=small[:, N:], start=True, stop=True)
+        bias_bc = const.tile([P, N], F32)
+        nc.vector.tensor_copy(
+            out=bias_bc[:].rearrange("q (j p) -> q j p", j=PACK),
+            in_=bias_ps[:].rearrange("q (p j) -> q j p", j=PACK),
+        )
+        gamma_bc = const.tile([P, 1], F32)
+        nc.vector.tensor_copy(out=gamma_bc[:], in_=gamma_ps[:, 0:1])
+
+        def new_mx_operand(name):
+            codes = quantised.tile([P, N], U32, tag=name + "_codes", name=name + "_codes", align_bytes=64)
+            scales = quantised.tile([P, N], U8, tag=name + "_scales", name=name + "_scales", align_bytes=64)
+            return codes, scales
+
+        def quantise(operand, values):
+            codes, scales = operand
+            nc.vector.quantize_mx(out=codes[:].bitcast(FP8X4), scales=scales[:], in_=values[:])
+
+        def mx_pass(acc, stationary, s_cols, moving, m_cols):
+            nc.tensor.matmul_mx(
+                out=acc,
+                lhsT=stationary[0][:, s_cols].bitcast(FP8X4),
+                lhsT_scale=stationary[1][:, s_cols],
+                rhs=moving[0][:, m_cols].bitcast(FP8X4),
+                rhs_scale=moving[1][:, m_cols],
+                start=True,
+                stop=True,
+            )
+
+        def features_onto_partitions(rows_sb, name, copy):
+            words = rows_sb[:].bitcast(F32)
+            values = grouped.tile([P, PACK * N], BF16, tag=name, name=name, align_bytes=64)
+            value_words = values[:].bitcast(F32).rearrange("q (c u) -> q c u", u=PAIR)
+            for half in range(2):
+                flip = flip_psum.tile([P, PAIR, 2 * P], F32, tag="flip")
+                for jj in range(2):
+                    for u in range(PAIR):
+                        first = (2 * half + jj) * (N // PAIR) + u * P
+                        nc.tensor.transpose(
+                            flip[:, u, jj * P : (jj + 1) * P], words[:, first : first + P], ident[:]
+                        )
+                copy(
+                    out=value_words[:, half * 2 * P : (half + 1) * 2 * P, :],
+                    in_=flip[:].rearrange("q u c -> q c u"),
+                )
+            return values
+
+        w_mx = new_mx_operand("w")
+        quantise(w_mx, features_onto_partitions(w_sb, "w_values", nc.vector.tensor_copy))
+
+        x_values, att_values, v_values = {}, {}, {}
+        x_mx, att_mx, v_mx = {}, {}, {}
+
+        def prepare(b):
+            x_values[b] = features_onto_partitions(x_in[b], "x_values", nc.scalar.copy)
+            att_values[b] = grouped.tile([P, PACK * N], BF16, tag="att_values", name="att_values", align_bytes=64)
+            nc.scalar.copy(
+                out=att_values[b][:].rearrange("p (c i j) -> p c j i", i=4, j=PACK),
+                in_=att_in[b][:].rearrange("p (j c i) -> p c j i", j=PACK, i=4),
+            )
+
+        def quantise_inputs(b):
+            x_mx[b] = new_mx_operand("x")
+            quantise(x_mx[b], x_values[b])
+            att_mx[b] = new_mx_operand("att")
+            quantise(att_mx[b], att_values[b])
+
+        def project(b):
+            v_values[b] = grouped.tile([P, PACK * N], BF16, tag="v_values", name="v_values", align_bytes=64)
+            for i in range(PACK):
+                cols = slice(i * P, (i + 1) * P)
+                v_ps = v_psum.tile([P, PACK, P], F32)
+                for t in range(PACK):
+                    mx_pass(v_ps[:, t, :], x_mx[b], slice(t * P, (t + 1) * P), w_mx, cols)
+                nc.vector.tensor_tensor(
+                    out=v_values[b][:, i * PACK * P : (i + 1) * PACK * P].rearrange("p (d t) -> p d t", t=PACK),
+                    in0=v_ps[:].rearrange("p t d -> p d t"),
+                    in1=bias_bc[:, cols].unsqueeze(2).to_broadcast([P, P, PACK]),
+                    op=ADD,
+                )
+
+        def quantise_v(b):
+            v_mx[b] = new_mx_operand("v")
+            quantise(v_mx[b], v_values[b])
+
+        def attend(b):
+            res = results.tile([P, PACK * N], F32)
+            for c in range(PACK):
+                o_ps = o_psum.tile([P, N], F32)
+                mx_pass(o_ps[:], v_mx[b], slice(c * P, (c + 1) * P), att_mx[b], slice(0, N))
+                nc.vector.scalar_tensor_tensor(
+                    out=res[:, c * N : (c + 1) * N],
+                    in0=o_ps[:],
+                    scalar=gamma_bc[:, 0:1],
+                    in1=y_in[b][:, c * N : (c + 1) * N],
+                    op0=MULT,
+                    op1=ADD,
+                )
+            nc.sync.dma_start(out=out[b].rearrange("(p c) m -> p (c m)", c=PACK), in_=res[:])
+
+        for i in range(-2, B + 1):
+            if 0 <= i < B:
+                project(i)
+            if 0 <= i + 2 < B:
+                prepare(i + 2)
+            if 0 <= i + 1 < B:
+                quantise_inputs(i + 1)
+            if 0 <= i < B:
+                quantise_v(i)
+            if 0 <= i - 1 < B:
+                attend(i - 1)

@@ -10,12 +10,14 @@ U8 = mybir.dt.uint8
 FP8X4 = mybir.dt.float8_e4m3fn_x4
 ADD = mybir.AluOpType.add
 MULT = mybir.AluOpType.mult
+COPY = mybir.ActivationFunctionType.Copy
 
 B = 8
 N = 512
 P = 128
 PACK = 4
 PAIR = 2
+AHEAD = 2
 GAMMA_COLS = 64
 
 FLOPS = 2 * B * (N * N * N + N * N * N)
@@ -24,17 +26,17 @@ FLOPS = 2 * B * (N * N * N + N * N * N)
 def tile_dualcrossmodalattention_pb_t_kernel(tc, x, Wv1, bv1, att2, gamma2, y, out):
     nc = tc.nc
     with ExitStack() as ctx:
+        ctx.enter_context(tc.manual_schedule())
         const = ctx.enter_context(tc.tile_pool(name="const", bufs=1))
         inputs = ctx.enter_context(tc.tile_pool(name="inputs", bufs=B))
         grouped = ctx.enter_context(tc.tile_pool(name="grouped", bufs=2))
-        quantised = ctx.enter_context(tc.tile_pool(name="quantised", bufs=3))
-        results = ctx.enter_context(tc.tile_pool(name="results", bufs=3))
+        quantised = ctx.enter_context(tc.tile_pool(name="quantised", bufs=2))
+        results = ctx.enter_context(tc.tile_pool(name="results", bufs=4))
         flip_psum = ctx.enter_context(tc.psum_pool(name="flip_psum", bufs=2))
-        v_psum = ctx.enter_context(tc.psum_pool(name="v_psum", bufs=3))
-        o_psum = ctx.enter_context(tc.psum_pool(name="o_psum", bufs=3))
+        acc_psum = ctx.enter_context(tc.psum_pool(name="acc_psum", bufs=6))
 
-        def load_rows(matrix, name):
-            rows_sb = inputs.tile([P, PACK * N], BF16, tag=name, name=name)
+        def load_rows(pool, matrix, name):
+            rows_sb = pool.tile([P, PACK * N], BF16, tag=name, name=name)
             nc.sync.dma_start(out=rows_sb[:], in_=matrix.rearrange("(p j) c -> p (j c)", j=PACK))
             return rows_sb
 
@@ -42,22 +44,26 @@ def tile_dualcrossmodalattention_pb_t_kernel(tc, x, Wv1, bv1, att2, gamma2, y, o
         nc.vector.memset(small[:], 0.0)
         nc.sync.dma_start(out=small[0:1, 0:N], in_=bv1.rearrange("(o d) -> o d", o=1))
         nc.sync.dma_start(out=small[0:1, N : N + 1], in_=gamma2.rearrange("(o g) -> o g", o=1))
-        w_sb = const.tile([P, PACK * N], BF16)
-        nc.sync.dma_start(out=w_sb[:], in_=Wv1.rearrange("(p j) c -> p (j c)", j=PACK))
-        x_in, att_in, y_in = [], [], []
+        w_sb = load_rows(const, Wv1, "w_sb")
+        x_in, att_in, y_in = {}, {}, {}
+        for b in range(AHEAD):
+            x_in[b] = load_rows(inputs, x[b], "x_sb")
+        for b in range(AHEAD):
+            att_in[b] = load_rows(inputs, att2[b], "att_sb")
         for b in range(B):
-            x_in.append(load_rows(x[b], "x_sb"))
-            att_in.append(load_rows(att2[b], "att_sb"))
-            y_in.append(load_rows(y[b], "y_sb"))
+            if b + AHEAD < B:
+                x_in[b + AHEAD] = load_rows(inputs, x[b + AHEAD], "x_sb")
+                att_in[b + AHEAD] = load_rows(inputs, att2[b + AHEAD], "att_sb")
+            y_in[b] = load_rows(inputs, y[b], "y_sb")
 
         ident = const.tile([P, P], F32)
         make_identity(nc, ident[:])
         ones = const.tile([P, P], BF16)
         nc.vector.memset(ones[:], 1.0)
 
-        bias_ps = flip_psum.tile([P, N], F32, tag="flip")
+        bias_ps = acc_psum.tile([P, N], F32, tag="acc")
         nc.tensor.matmul(out=bias_ps[:], lhsT=ones[:], rhs=small[:, 0:N], start=True, stop=True)
-        gamma_ps = flip_psum.tile([P, GAMMA_COLS], F32, tag="flip")
+        gamma_ps = acc_psum.tile([P, GAMMA_COLS], F32, tag="acc")
         nc.tensor.matmul(out=gamma_ps[:], lhsT=ones[:], rhs=small[:, N:], start=True, stop=True)
         bias_bc = const.tile([P, N], F32)
         nc.vector.tensor_copy(
@@ -67,14 +73,11 @@ def tile_dualcrossmodalattention_pb_t_kernel(tc, x, Wv1, bv1, att2, gamma2, y, o
         gamma_bc = const.tile([P, 1], F32)
         nc.vector.tensor_copy(out=gamma_bc[:], in_=gamma_ps[:, 0:1])
 
-        def new_mx_operand(name):
-            codes = quantised.tile([P, N], U32, tag=name + "_codes", name=name + "_codes", align_bytes=64)
-            scales = quantised.tile([P, N], U8, tag=name + "_scales", name=name + "_scales", align_bytes=64)
-            return codes, scales
-
-        def quantise(operand, values):
-            codes, scales = operand
+        def quantise(pool, name, values):
+            codes = pool.tile([P, N], U32, tag=name + "_codes", name=name + "_codes", align_bytes=64)
+            scales = pool.tile([P, N], U8, tag=name + "_scales", name=name + "_scales", align_bytes=64)
             nc.vector.quantize_mx(out=codes[:].bitcast(FP8X4), scales=scales[:], in_=values[:])
+            return codes, scales
 
         def mx_pass(acc, stationary, s_cols, moving, m_cols):
             nc.tensor.matmul_mx(
@@ -87,49 +90,48 @@ def tile_dualcrossmodalattention_pb_t_kernel(tc, x, Wv1, bv1, att2, gamma2, y, o
                 stop=True,
             )
 
-        def features_onto_partitions(rows_sb, name, copy):
+        def transpose_words(rows_sb):
             words = rows_sb[:].bitcast(F32)
-            values = grouped.tile([P, PACK * N], BF16, tag=name, name=name, align_bytes=64)
-            value_words = values[:].bitcast(F32).rearrange("q (c u) -> q c u", u=PAIR)
-            for half in range(2):
+            flips = []
+            for first_group in (0, 2):
                 flip = flip_psum.tile([P, PAIR, 2 * P], F32, tag="flip")
                 for jj in range(2):
                     for u in range(PAIR):
-                        first = (2 * half + jj) * (N // PAIR) + u * P
+                        first = (first_group + jj) * (N // PAIR) + u * P
                         nc.tensor.transpose(
                             flip[:, u, jj * P : (jj + 1) * P], words[:, first : first + P], ident[:]
                         )
+                flips.append(flip)
+            return flips
+
+        def interleave_halves(pool, name, flips, copy):
+            values = pool.tile([P, PACK * N], BF16, tag=name, name=name, align_bytes=64)
+            value_words = values[:].bitcast(F32).rearrange("q (c u) -> q c u", u=PAIR)
+            for h in range(2):
                 copy(
-                    out=value_words[:, half * 2 * P : (half + 1) * 2 * P, :],
-                    in_=flip[:].rearrange("q u c -> q c u"),
+                    out=value_words[:, h * 2 * P : (h + 1) * 2 * P, :],
+                    in_=flips[h][:].rearrange("q u c -> q c u"),
                 )
             return values
 
-        w_mx = new_mx_operand("w")
-        quantise(w_mx, features_onto_partitions(w_sb, "w_values", nc.vector.tensor_copy))
+        w_values = interleave_halves(const, "w_values", transpose_words(w_sb), nc.vector.tensor_copy)
+        w_mx = quantise(const, "w", w_values)
 
-        x_values, att_values, v_values = {}, {}, {}
+        x_flips, x_values, att_values, v_values = {}, {}, {}, {}
         x_mx, att_mx, v_mx = {}, {}, {}
 
-        def prepare(b):
-            x_values[b] = features_onto_partitions(x_in[b], "x_values", nc.scalar.copy)
+        def regroup_att(b):
             att_values[b] = grouped.tile([P, PACK * N], BF16, tag="att_values", name="att_values", align_bytes=64)
             nc.scalar.copy(
                 out=att_values[b][:].rearrange("p (c i j) -> p c j i", i=4, j=PACK),
                 in_=att_in[b][:].rearrange("p (j c i) -> p c j i", j=PACK, i=4),
             )
 
-        def quantise_inputs(b):
-            x_mx[b] = new_mx_operand("x")
-            quantise(x_mx[b], x_values[b])
-            att_mx[b] = new_mx_operand("att")
-            quantise(att_mx[b], att_values[b])
-
         def project(b):
             v_values[b] = grouped.tile([P, PACK * N], BF16, tag="v_values", name="v_values", align_bytes=64)
             for i in range(PACK):
                 cols = slice(i * P, (i + 1) * P)
-                v_ps = v_psum.tile([P, PACK, P], F32)
+                v_ps = acc_psum.tile([P, PACK, P], F32, tag="acc")
                 for t in range(PACK):
                     mx_pass(v_ps[:, t, :], x_mx[b], slice(t * P, (t + 1) * P), w_mx, cols)
                 nc.vector.tensor_tensor(
@@ -139,33 +141,37 @@ def tile_dualcrossmodalattention_pb_t_kernel(tc, x, Wv1, bv1, att2, gamma2, y, o
                     op=ADD,
                 )
 
-        def quantise_v(b):
-            v_mx[b] = new_mx_operand("v")
-            quantise(v_mx[b], v_values[b])
-
         def attend(b):
-            res = results.tile([P, PACK * N], F32)
+            out_rows = out[b].rearrange("(p c) m -> p c m", c=PACK)
+            res_g = results.tile([P, 2, N], F32)
+            res_v = results.tile([P, 2, N], F32)
             for c in range(PACK):
-                o_ps = o_psum.tile([P, N], F32)
+                o_ps = acc_psum.tile([P, N], F32, tag="acc")
                 mx_pass(o_ps[:], v_mx[b], slice(c * P, (c + 1) * P), att_mx[b], slice(0, N))
-                nc.vector.scalar_tensor_tensor(
-                    out=res[:, c * N : (c + 1) * N],
-                    in0=o_ps[:],
-                    scalar=gamma_bc[:, 0:1],
-                    in1=y_in[b][:, c * N : (c + 1) * N],
-                    op0=MULT,
-                    op1=ADD,
-                )
-            nc.sync.dma_start(out=out[b].rearrange("(p c) m -> p (c m)", c=PACK), in_=res[:])
+                y_rows = y_in[b][:, c * N : (c + 1) * N]
+                if c < 2:
+                    nc.scalar.activation(out=res_g[:, c, :], in_=o_ps[:], func=COPY, scale=gamma_bc[:, 0:1])
+                    nc.gpsimd.tensor_tensor(out=res_g[:, c, :], in0=res_g[:, c, :], in1=y_rows, op=ADD)
+                else:
+                    nc.vector.scalar_tensor_tensor(
+                        out=res_v[:, c - 2, :], in0=o_ps[:], scalar=gamma_bc[:, 0:1], in1=y_rows, op0=MULT, op1=ADD
+                    )
+            nc.sync.dma_start(out=out_rows[:, 0:2, :], in_=res_g[:])
+            nc.sync.dma_start(out=out_rows[:, 2:4, :], in_=res_v[:])
 
-        for i in range(-2, B + 1):
-            if 0 <= i < B:
-                project(i)
-            if 0 <= i + 2 < B:
-                prepare(i + 2)
+        for i in range(-AHEAD, B):
+            if i + 2 < B:
+                x_flips[i + 2] = transpose_words(x_in[i + 2])
+            if 0 <= i:
+                att_mx[i] = quantise(quantised, "att", att_values[i])
             if 0 <= i + 1 < B:
-                quantise_inputs(i + 1)
-            if 0 <= i < B:
-                quantise_v(i)
-            if 0 <= i - 1 < B:
-                attend(i - 1)
+                x_mx[i + 1] = quantise(quantised, "x", x_values[i + 1])
+            if 0 <= i:
+                v_mx[i] = quantise(quantised, "v", v_values[i])
+            if 0 <= i + 1 < B:
+                project(i + 1)
+            if 0 <= i:
+                attend(i)
+            if i + 2 < B:
+                x_values[i + 2] = interleave_halves(grouped, "x_values", x_flips[i + 2], nc.scalar.copy)
+                regroup_att(i + 2)

@@ -17,7 +17,8 @@ N = 512
 P = 128
 PACK = 4
 PAIR = 2
-AHEAD = 2
+X_AHEAD = 4
+ATT_AHEAD = 2
 GAMMA_COLS = 64
 
 FLOPS = 2 * B * (N * N * N + N * N * N)
@@ -31,7 +32,7 @@ def tile_dualcrossmodalattention_pb_t_kernel(tc, x, Wv1, bv1, att2, gamma2, y, o
         inputs = ctx.enter_context(tc.tile_pool(name="inputs", bufs=B))
         grouped = ctx.enter_context(tc.tile_pool(name="grouped", bufs=2))
         quantised = ctx.enter_context(tc.tile_pool(name="quantised", bufs=2))
-        results = ctx.enter_context(tc.tile_pool(name="results", bufs=4))
+        results = ctx.enter_context(tc.tile_pool(name="results", bufs=8))
         flip_psum = ctx.enter_context(tc.psum_pool(name="flip_psum", bufs=2))
         acc_psum = ctx.enter_context(tc.psum_pool(name="acc_psum", bufs=6))
 
@@ -46,15 +47,13 @@ def tile_dualcrossmodalattention_pb_t_kernel(tc, x, Wv1, bv1, att2, gamma2, y, o
         nc.sync.dma_start(out=small[0:1, N : N + 1], in_=gamma2.rearrange("(o g) -> o g", o=1))
         w_sb = load_rows(const, Wv1, "w_sb")
         x_in, att_in, y_in = {}, {}, {}
-        for b in range(AHEAD):
-            x_in[b] = load_rows(inputs, x[b], "x_sb")
-        for b in range(AHEAD):
-            att_in[b] = load_rows(inputs, att2[b], "att_sb")
-        for b in range(B):
-            if b + AHEAD < B:
-                x_in[b + AHEAD] = load_rows(inputs, x[b + AHEAD], "x_sb")
-                att_in[b + AHEAD] = load_rows(inputs, att2[b + AHEAD], "att_sb")
-            y_in[b] = load_rows(inputs, y[b], "y_sb")
+        for i in range(-X_AHEAD, B):
+            if i + X_AHEAD < B:
+                x_in[i + X_AHEAD] = load_rows(inputs, x[i + X_AHEAD], "x_sb")
+            if 0 <= i + ATT_AHEAD < B:
+                att_in[i + ATT_AHEAD] = load_rows(inputs, att2[i + ATT_AHEAD], "att_sb")
+            if 0 <= i:
+                y_in[i] = load_rows(inputs, y[i], "y_sb")
 
         ident = const.tile([P, P], F32)
         make_identity(nc, ident[:])
@@ -117,7 +116,7 @@ def tile_dualcrossmodalattention_pb_t_kernel(tc, x, Wv1, bv1, att2, gamma2, y, o
         w_values = interleave_halves(const, "w_values", transpose_words(w_sb), nc.vector.tensor_copy)
         w_mx = quantise(const, "w", w_values)
 
-        x_flips, x_values, att_values, v_values = {}, {}, {}, {}
+        x_flips, x_values, att_values, v_banks, v_values = {}, {}, {}, {}, {}
         x_mx, att_mx, v_mx = {}, {}, {}
 
         def regroup_att(b):
@@ -128,50 +127,58 @@ def tile_dualcrossmodalattention_pb_t_kernel(tc, x, Wv1, bv1, att2, gamma2, y, o
             )
 
         def project(b):
-            v_values[b] = grouped.tile([P, PACK * N], BF16, tag="v_values", name="v_values", align_bytes=64)
+            banks = []
             for i in range(PACK):
-                cols = slice(i * P, (i + 1) * P)
                 v_ps = acc_psum.tile([P, PACK, P], F32, tag="acc")
                 for t in range(PACK):
-                    mx_pass(v_ps[:, t, :], x_mx[b], slice(t * P, (t + 1) * P), w_mx, cols)
+                    mx_pass(v_ps[:, t, :], x_mx[b], slice(t * P, (t + 1) * P), w_mx, slice(i * P, (i + 1) * P))
+                banks.append(v_ps)
+            return banks
+
+        def add_bias(b):
+            v_values[b] = grouped.tile([P, PACK * N], BF16, tag="v_values", name="v_values", align_bytes=64)
+            for i in range(PACK):
                 nc.vector.tensor_tensor(
                     out=v_values[b][:, i * PACK * P : (i + 1) * PACK * P].rearrange("p (d t) -> p d t", t=PACK),
-                    in0=v_ps[:].rearrange("p t d -> p d t"),
-                    in1=bias_bc[:, cols].unsqueeze(2).to_broadcast([P, P, PACK]),
+                    in0=v_banks[b][i][:].rearrange("p t d -> p d t"),
+                    in1=bias_bc[:, i * P : (i + 1) * P].unsqueeze(2).to_broadcast([P, P, PACK]),
                     op=ADD,
                 )
 
-        def attend(b):
-            out_rows = out[b].rearrange("(p c) m -> p c m", c=PACK)
-            res_g = results.tile([P, 2, N], F32)
-            res_v = results.tile([P, 2, N], F32)
-            for c in range(PACK):
+        def attend(b, first_group, on_vector):
+            res = results.tile([P, 2, N], F32)
+            for h in range(2):
+                c = first_group + h
                 o_ps = acc_psum.tile([P, N], F32, tag="acc")
                 mx_pass(o_ps[:], v_mx[b], slice(c * P, (c + 1) * P), att_mx[b], slice(0, N))
                 y_rows = y_in[b][:, c * N : (c + 1) * N]
-                if c < 2:
-                    nc.scalar.activation(out=res_g[:, c, :], in_=o_ps[:], func=COPY, scale=gamma_bc[:, 0:1])
-                    nc.gpsimd.tensor_tensor(out=res_g[:, c, :], in0=res_g[:, c, :], in1=y_rows, op=ADD)
-                else:
+                if on_vector:
                     nc.vector.scalar_tensor_tensor(
-                        out=res_v[:, c - 2, :], in0=o_ps[:], scalar=gamma_bc[:, 0:1], in1=y_rows, op0=MULT, op1=ADD
+                        out=res[:, h, :], in0=o_ps[:], scalar=gamma_bc[:, 0:1], in1=y_rows, op0=MULT, op1=ADD
                     )
-            nc.sync.dma_start(out=out_rows[:, 0:2, :], in_=res_g[:])
-            nc.sync.dma_start(out=out_rows[:, 2:4, :], in_=res_v[:])
+                else:
+                    nc.scalar.activation(out=res[:, h, :], in_=o_ps[:], func=COPY, scale=gamma_bc[:, 0:1])
+                    nc.gpsimd.tensor_tensor(out=res[:, h, :], in0=res[:, h, :], in1=y_rows, op=ADD)
+            out_rows = out[b].rearrange("(p c) m -> p c m", c=PACK)
+            nc.sync.dma_start(out=out_rows[:, first_group : first_group + 2, :], in_=res[:])
 
-        for i in range(-AHEAD, B):
-            if i + 2 < B:
-                x_flips[i + 2] = transpose_words(x_in[i + 2])
+        for i in range(-X_AHEAD, B):
             if 0 <= i:
                 att_mx[i] = quantise(quantised, "att", att_values[i])
-            if 0 <= i + 1 < B:
-                x_mx[i + 1] = quantise(quantised, "x", x_values[i + 1])
+            if 0 <= i + 2 < B:
+                x_mx[i + 2] = quantise(quantised, "x", x_values[i + 2])
             if 0 <= i:
                 v_mx[i] = quantise(quantised, "v", v_values[i])
+                attend(i, 0, False)
             if 0 <= i + 1 < B:
-                project(i + 1)
+                add_bias(i + 1)
             if 0 <= i:
-                attend(i)
-            if i + 2 < B:
-                x_values[i + 2] = interleave_halves(grouped, "x_values", x_flips[i + 2], nc.scalar.copy)
-                regroup_att(i + 2)
+                attend(i, 2, True)
+            if 0 <= i + 2 < B:
+                v_banks[i + 2] = project(i + 2)
+            if 0 <= i + 3 < B:
+                x_values[i + 3] = interleave_halves(grouped, "x_values", x_flips[i + 3], nc.scalar.copy)
+            if i + X_AHEAD < B:
+                x_flips[i + X_AHEAD] = transpose_words(x_in[i + X_AHEAD])
+            if 0 <= i + ATT_AHEAD < B:
+                regroup_att(i + ATT_AHEAD)

@@ -32,7 +32,7 @@ def tile_dualcrossmodalattention_pb_t_kernel(tc, x, Wv1, bv1, att2, gamma2, y, o
         inputs = ctx.enter_context(tc.tile_pool(name="inputs", bufs=B))
         grouped = ctx.enter_context(tc.tile_pool(name="grouped", bufs=2))
         quantised = ctx.enter_context(tc.tile_pool(name="quantised", bufs=2))
-        results = ctx.enter_context(tc.tile_pool(name="results", bufs=8))
+        results = ctx.enter_context(tc.tile_pool(name="results", bufs=16))
         flip_psum = ctx.enter_context(tc.psum_pool(name="flip_psum", bufs=2))
         acc_psum = ctx.enter_context(tc.psum_pool(name="acc_psum", bufs=6))
 
@@ -43,13 +43,14 @@ def tile_dualcrossmodalattention_pb_t_kernel(tc, x, Wv1, bv1, att2, gamma2, y, o
 
         small = const.tile([P, N + GAMMA_COLS], BF16)
         nc.vector.memset(small[:], 0.0)
-        nc.sync.dma_start(out=small[0:1, 0:N], in_=bv1.rearrange("(o d) -> o d", o=1))
-        nc.sync.dma_start(out=small[0:1, N : N + 1], in_=gamma2.rearrange("(o g) -> o g", o=1))
         w_sb = load_rows(const, Wv1, "w_sb")
         x_in, att_in, y_in = {}, {}, {}
         for i in range(-X_AHEAD, B):
             if i + X_AHEAD < B:
                 x_in[i + X_AHEAD] = load_rows(inputs, x[i + X_AHEAD], "x_sb")
+            if i == -X_AHEAD:
+                nc.sync.dma_start(out=small[0:1, 0:N], in_=bv1.rearrange("(o d) -> o d", o=1))
+                nc.sync.dma_start(out=small[0:1, N : N + 1], in_=gamma2.rearrange("(o g) -> o g", o=1))
             if 0 <= i + ATT_AHEAD < B:
                 att_in[i + ATT_AHEAD] = load_rows(inputs, att2[i + ATT_AHEAD], "att_sb")
             if 0 <= i:
@@ -59,18 +60,6 @@ def tile_dualcrossmodalattention_pb_t_kernel(tc, x, Wv1, bv1, att2, gamma2, y, o
         make_identity(nc, ident[:])
         ones = const.tile([P, P], BF16)
         nc.vector.memset(ones[:], 1.0)
-
-        bias_ps = acc_psum.tile([P, N], F32, tag="acc")
-        nc.tensor.matmul(out=bias_ps[:], lhsT=ones[:], rhs=small[:, 0:N], start=True, stop=True)
-        gamma_ps = acc_psum.tile([P, GAMMA_COLS], F32, tag="acc")
-        nc.tensor.matmul(out=gamma_ps[:], lhsT=ones[:], rhs=small[:, N:], start=True, stop=True)
-        bias_bc = const.tile([P, N], F32)
-        nc.vector.tensor_copy(
-            out=bias_bc[:].rearrange("q (j p) -> q j p", j=PACK),
-            in_=bias_ps[:].rearrange("q (p j) -> q j p", j=PACK),
-        )
-        gamma_bc = const.tile([P, 1], F32)
-        nc.vector.tensor_copy(out=gamma_bc[:], in_=gamma_ps[:, 0:1])
 
         def quantise(pool, name, values):
             codes = pool.tile([P, N], U32, tag=name + "_codes", name=name + "_codes", align_bytes=64)
@@ -89,11 +78,11 @@ def tile_dualcrossmodalattention_pb_t_kernel(tc, x, Wv1, bv1, att2, gamma2, y, o
                 stop=True,
             )
 
-        def transpose_words(rows_sb):
+        def transpose_words(rows_sb, pool, tag):
             words = rows_sb[:].bitcast(F32)
             flips = []
             for first_group in (0, 2):
-                flip = flip_psum.tile([P, PAIR, 2 * P], F32, tag="flip")
+                flip = pool.tile([P, PAIR, 2 * P], F32, tag=tag)
                 for jj in range(2):
                     for u in range(PAIR):
                         first = (first_group + jj) * (N // PAIR) + u * P
@@ -113,10 +102,24 @@ def tile_dualcrossmodalattention_pb_t_kernel(tc, x, Wv1, bv1, att2, gamma2, y, o
                 )
             return values
 
-        w_values = interleave_halves(const, "w_values", transpose_words(w_sb), nc.vector.tensor_copy)
+        w_values = interleave_halves(const, "w_values", transpose_words(w_sb, acc_psum, "acc"), nc.vector.tensor_copy)
         w_mx = quantise(const, "w", w_values)
 
-        x_flips, x_values, att_values, v_banks, v_values = {}, {}, {}, {}, {}
+        x_flips = {0: transpose_words(x_in[0], flip_psum, "flip")}
+
+        bias_ps = acc_psum.tile([P, N], F32, tag="acc")
+        nc.tensor.matmul(out=bias_ps[:], lhsT=ones[:], rhs=small[:, 0:N], start=True, stop=True)
+        gamma_ps = acc_psum.tile([P, GAMMA_COLS], F32, tag="acc")
+        nc.tensor.matmul(out=gamma_ps[:], lhsT=ones[:], rhs=small[:, N:], start=True, stop=True)
+        bias_bc = const.tile([P, N], F32)
+        nc.vector.tensor_copy(
+            out=bias_bc[:].rearrange("q (j p) -> q j p", j=PACK),
+            in_=bias_ps[:].rearrange("q (p j) -> q j p", j=PACK),
+        )
+        gamma_bc = const.tile([P, 1], F32)
+        nc.vector.tensor_copy(out=gamma_bc[:], in_=gamma_ps[:, 0:1])
+
+        x_values, att_values, v_banks, v_values = {}, {}, {}, {}
         x_mx, att_mx, v_mx = {}, {}, {}
 
         def regroup_att(b):
@@ -145,40 +148,40 @@ def tile_dualcrossmodalattention_pb_t_kernel(tc, x, Wv1, bv1, att2, gamma2, y, o
                     op=ADD,
                 )
 
-        def attend(b, first_group, on_vector):
-            res = results.tile([P, 2, N], F32)
-            for h in range(2):
-                c = first_group + h
-                o_ps = acc_psum.tile([P, N], F32, tag="acc")
-                mx_pass(o_ps[:], v_mx[b], slice(c * P, (c + 1) * P), att_mx[b], slice(0, N))
-                y_rows = y_in[b][:, c * N : (c + 1) * N]
-                if on_vector:
-                    nc.vector.scalar_tensor_tensor(
-                        out=res[:, h, :], in0=o_ps[:], scalar=gamma_bc[:, 0:1], in1=y_rows, op0=MULT, op1=ADD
-                    )
-                else:
-                    nc.scalar.activation(out=res[:, h, :], in_=o_ps[:], func=COPY, scale=gamma_bc[:, 0:1])
-                    nc.gpsimd.tensor_tensor(out=res[:, h, :], in0=res[:, h, :], in1=y_rows, op=ADD)
-            out_rows = out[b].rearrange("(p c) m -> p c m", c=PACK)
-            nc.sync.dma_start(out=out_rows[:, first_group : first_group + 2, :], in_=res[:])
+        def attend(b, c, on_vector):
+            o_ps = acc_psum.tile([P, N], F32, tag="acc")
+            mx_pass(o_ps[:], v_mx[b], slice(c * P, (c + 1) * P), att_mx[b], slice(0, N))
+            y_rows = y_in[b][:, c * N : (c + 1) * N]
+            res = results.tile([P, N], F32)
+            if on_vector:
+                nc.vector.scalar_tensor_tensor(
+                    out=res[:], in0=o_ps[:], scalar=gamma_bc[:, 0:1], in1=y_rows, op0=MULT, op1=ADD
+                )
+            else:
+                nc.scalar.activation(out=res[:], in_=o_ps[:], func=COPY, scale=gamma_bc[:, 0:1])
+                nc.gpsimd.tensor_tensor(out=res[:], in0=res[:], in1=y_rows, op=ADD)
+            nc.sync.dma_start(out=out[b].rearrange("(p c) m -> p c m", c=PACK)[:, c, :], in_=res[:])
 
-        for i in range(-X_AHEAD, B):
+        for i in range(1 - X_AHEAD, B):
             if 0 <= i:
                 att_mx[i] = quantise(quantised, "att", att_values[i])
             if 0 <= i + 2 < B:
                 x_mx[i + 2] = quantise(quantised, "x", x_values[i + 2])
             if 0 <= i:
                 v_mx[i] = quantise(quantised, "v", v_values[i])
-                attend(i, 0, False)
+                handed_over = 2 if i + 1 < B else 1
+                for c in range(handed_over):
+                    attend(i, c, False)
             if 0 <= i + 1 < B:
                 add_bias(i + 1)
             if 0 <= i:
-                attend(i, 2, True)
+                for c in range(handed_over, PACK):
+                    attend(i, c, True)
             if 0 <= i + 2 < B:
                 v_banks[i + 2] = project(i + 2)
             if 0 <= i + 3 < B:
                 x_values[i + 3] = interleave_halves(grouped, "x_values", x_flips[i + 3], nc.scalar.copy)
             if i + X_AHEAD < B:
-                x_flips[i + X_AHEAD] = transpose_words(x_in[i + X_AHEAD])
+                x_flips[i + X_AHEAD] = transpose_words(x_in[i + X_AHEAD], flip_psum, "flip")
             if 0 <= i + ATT_AHEAD < B:
                 regroup_att(i + ATT_AHEAD)

@@ -17,9 +17,13 @@ N = 512
 P = 128
 PACK = 4
 PAIR = 2
-X_AHEAD = 4
-ATT_AHEAD = 2
+PSUM_BANKS = 8
 GAMMA_COLS = 64
+
+TRANSPOSE_AHEAD = 4
+COPY_AHEAD = 3
+PROJECT_AHEAD = 2
+BIAS_AHEAD = 1
 
 FLOPS = 2 * B * (N * N * N + N * N * N)
 
@@ -32,27 +36,26 @@ def tile_dualcrossmodalattention_pb_t_kernel(tc, x, Wv1, bv1, att2, gamma2, y, o
         inputs = ctx.enter_context(tc.tile_pool(name="inputs", bufs=B))
         grouped = ctx.enter_context(tc.tile_pool(name="grouped", bufs=2))
         quantised = ctx.enter_context(tc.tile_pool(name="quantised", bufs=2))
-        results = ctx.enter_context(tc.tile_pool(name="results", bufs=16))
-        flip_psum = ctx.enter_context(tc.psum_pool(name="flip_psum", bufs=2))
-        acc_psum = ctx.enter_context(tc.psum_pool(name="acc_psum", bufs=6))
+        results = ctx.enter_context(tc.tile_pool(name="results", bufs=4 * PACK))
+        psum = ctx.enter_context(tc.psum_pool(name="psum", bufs=PSUM_BANKS))
 
         def load_rows(pool, matrix, name):
             rows_sb = pool.tile([P, PACK * N], BF16, tag=name, name=name)
             nc.sync.dma_start(out=rows_sb[:], in_=matrix.rearrange("(p j) c -> p (j c)", j=PACK))
             return rows_sb
 
+        x_in, att_in, y_in = {}, {}, {}
+        w_sb = load_rows(const, Wv1, "w_sb")
+        x_in[0] = load_rows(inputs, x[0], "x_sb")
         small = const.tile([P, N + GAMMA_COLS], BF16)
         nc.vector.memset(small[:], 0.0)
-        w_sb = load_rows(const, Wv1, "w_sb")
-        x_in, att_in, y_in = {}, {}, {}
-        for i in range(-X_AHEAD, B):
-            if i + X_AHEAD < B:
-                x_in[i + X_AHEAD] = load_rows(inputs, x[i + X_AHEAD], "x_sb")
-            if i == -X_AHEAD:
-                nc.sync.dma_start(out=small[0:1, 0:N], in_=bv1.rearrange("(o d) -> o d", o=1))
-                nc.sync.dma_start(out=small[0:1, N : N + 1], in_=gamma2.rearrange("(o g) -> o g", o=1))
-            if 0 <= i + ATT_AHEAD < B:
-                att_in[i + ATT_AHEAD] = load_rows(inputs, att2[i + ATT_AHEAD], "att_sb")
+        nc.sync.dma_start(out=small[0:1, 0:N], in_=bv1.rearrange("(o d) -> o d", o=1))
+        nc.sync.dma_start(out=small[0:1, N : N + 1], in_=gamma2.rearrange("(o g) -> o g", o=1))
+        for i in range(1 - TRANSPOSE_AHEAD, B):
+            if i + TRANSPOSE_AHEAD < B:
+                x_in[i + TRANSPOSE_AHEAD] = load_rows(inputs, x[i + TRANSPOSE_AHEAD], "x_sb")
+            if 0 <= i + PROJECT_AHEAD < B:
+                att_in[i + PROJECT_AHEAD] = load_rows(inputs, att2[i + PROJECT_AHEAD], "att_sb")
             if 0 <= i:
                 y_in[i] = load_rows(inputs, y[i], "y_sb")
 
@@ -78,11 +81,11 @@ def tile_dualcrossmodalattention_pb_t_kernel(tc, x, Wv1, bv1, att2, gamma2, y, o
                 stop=True,
             )
 
-        def transpose_words(rows_sb, pool, tag):
+        def transpose_words(rows_sb):
             words = rows_sb[:].bitcast(F32)
             flips = []
             for first_group in (0, 2):
-                flip = pool.tile([P, PAIR, 2 * P], F32, tag=tag)
+                flip = psum.tile([P, PAIR, 2 * P], F32, tag="bank")
                 for jj in range(2):
                     for u in range(PAIR):
                         first = (first_group + jj) * (N // PAIR) + u * P
@@ -102,14 +105,13 @@ def tile_dualcrossmodalattention_pb_t_kernel(tc, x, Wv1, bv1, att2, gamma2, y, o
                 )
             return values
 
-        w_values = interleave_halves(const, "w_values", transpose_words(w_sb, acc_psum, "acc"), nc.vector.tensor_copy)
+        w_values = interleave_halves(const, "w_values", transpose_words(w_sb), nc.vector.tensor_copy)
         w_mx = quantise(const, "w", w_values)
+        x_flips = {0: transpose_words(x_in[0])}
 
-        x_flips = {0: transpose_words(x_in[0], flip_psum, "flip")}
-
-        bias_ps = acc_psum.tile([P, N], F32, tag="acc")
+        bias_ps = psum.tile([P, N], F32, tag="bank")
         nc.tensor.matmul(out=bias_ps[:], lhsT=ones[:], rhs=small[:, 0:N], start=True, stop=True)
-        gamma_ps = acc_psum.tile([P, GAMMA_COLS], F32, tag="acc")
+        gamma_ps = psum.tile([P, GAMMA_COLS], F32, tag="bank")
         nc.tensor.matmul(out=gamma_ps[:], lhsT=ones[:], rhs=small[:, N:], start=True, stop=True)
         bias_bc = const.tile([P, N], F32)
         nc.vector.tensor_copy(
@@ -132,7 +134,7 @@ def tile_dualcrossmodalattention_pb_t_kernel(tc, x, Wv1, bv1, att2, gamma2, y, o
         def project(b):
             banks = []
             for i in range(PACK):
-                v_ps = acc_psum.tile([P, PACK, P], F32, tag="acc")
+                v_ps = psum.tile([P, PACK, P], F32, tag="bank")
                 for t in range(PACK):
                     mx_pass(v_ps[:, t, :], x_mx[b], slice(t * P, (t + 1) * P), w_mx, slice(i * P, (i + 1) * P))
                 banks.append(v_ps)
@@ -149,7 +151,7 @@ def tile_dualcrossmodalattention_pb_t_kernel(tc, x, Wv1, bv1, att2, gamma2, y, o
                 )
 
         def attend(b, c, on_vector):
-            o_ps = acc_psum.tile([P, N], F32, tag="acc")
+            o_ps = psum.tile([P, N], F32, tag="bank")
             mx_pass(o_ps[:], v_mx[b], slice(c * P, (c + 1) * P), att_mx[b], slice(0, N))
             y_rows = y_in[b][:, c * N : (c + 1) * N]
             res = results.tile([P, N], F32)
@@ -162,26 +164,29 @@ def tile_dualcrossmodalattention_pb_t_kernel(tc, x, Wv1, bv1, att2, gamma2, y, o
                 nc.gpsimd.tensor_tensor(out=res[:], in0=res[:], in1=y_rows, op=ADD)
             nc.sync.dma_start(out=out[b].rearrange("(p c) m -> p c m", c=PACK)[:, c, :], in_=res[:])
 
-        for i in range(1 - X_AHEAD, B):
-            if 0 <= i:
+        for i in range(1 - TRANSPOSE_AHEAD, B):
+            finishing = 0 <= i
+            if finishing:
                 att_mx[i] = quantise(quantised, "att", att_values[i])
-            if 0 <= i + 2 < B:
-                x_mx[i + 2] = quantise(quantised, "x", x_values[i + 2])
-            if 0 <= i:
+            if 0 <= i + PROJECT_AHEAD < B:
+                x_mx[i + PROJECT_AHEAD] = quantise(quantised, "x", x_values[i + PROJECT_AHEAD])
+            if finishing:
                 v_mx[i] = quantise(quantised, "v", v_values[i])
-                handed_over = 2 if i + 1 < B else 1
+                handed_over = 2 if i + BIAS_AHEAD < B else 1
                 for c in range(handed_over):
                     attend(i, c, False)
-            if 0 <= i + 1 < B:
-                add_bias(i + 1)
-            if 0 <= i:
+            if 0 <= i + BIAS_AHEAD < B:
+                add_bias(i + BIAS_AHEAD)
+            if finishing:
                 for c in range(handed_over, PACK):
                     attend(i, c, True)
-            if 0 <= i + 2 < B:
-                v_banks[i + 2] = project(i + 2)
-            if 0 <= i + 3 < B:
-                x_values[i + 3] = interleave_halves(grouped, "x_values", x_flips[i + 3], nc.scalar.copy)
-            if i + X_AHEAD < B:
-                x_flips[i + X_AHEAD] = transpose_words(x_in[i + X_AHEAD], flip_psum, "flip")
-            if 0 <= i + ATT_AHEAD < B:
-                regroup_att(i + ATT_AHEAD)
+            if 0 <= i + PROJECT_AHEAD < B:
+                v_banks[i + PROJECT_AHEAD] = project(i + PROJECT_AHEAD)
+            if 0 <= i + COPY_AHEAD < B:
+                x_values[i + COPY_AHEAD] = interleave_halves(
+                    grouped, "x_values", x_flips[i + COPY_AHEAD], nc.scalar.copy
+                )
+            if i + TRANSPOSE_AHEAD < B:
+                x_flips[i + TRANSPOSE_AHEAD] = transpose_words(x_in[i + TRANSPOSE_AHEAD])
+            if 0 <= i + PROJECT_AHEAD < B:
+                regroup_att(i + PROJECT_AHEAD)

@@ -168,10 +168,10 @@ def tile_dualcrossmodalattention_pb_t_kernel(tc, x, Wv1, bv1, att2, gamma2, y, o
             finishing = 0 <= i
             if finishing:
                 att_mx[i] = quantise(quantised, "att", att_values[i])
+                v_mx[i] = quantise(quantised, "v", v_values[i])
             if 0 <= i + PROJECT_AHEAD < B:
                 x_mx[i + PROJECT_AHEAD] = quantise(quantised, "x", x_values[i + PROJECT_AHEAD])
             if finishing:
-                v_mx[i] = quantise(quantised, "v", v_values[i])
                 handed_over = 2 if i + BIAS_AHEAD < B else 1
                 for c in range(handed_over):
                     attend(i, c, False)

@@ -17,13 +17,8 @@ N = 512
 P = 128
 PACK = 4
 PAIR = 2
-PSUM_BANKS = 8
+BANKS = {"flip": 2, "v": 4, "o": 2}
 GAMMA_COLS = 64
-
-TRANSPOSE_AHEAD = 4
-COPY_AHEAD = 3
-PROJECT_AHEAD = 2
-BIAS_AHEAD = 1
 
 FLOPS = 2 * B * (N * N * N + N * N * N)
 
@@ -34,10 +29,13 @@ def tile_dualcrossmodalattention_pb_t_kernel(tc, x, Wv1, bv1, att2, gamma2, y, o
         ctx.enter_context(tc.manual_schedule())
         const = ctx.enter_context(tc.tile_pool(name="const", bufs=1))
         inputs = ctx.enter_context(tc.tile_pool(name="inputs", bufs=B))
-        grouped = ctx.enter_context(tc.tile_pool(name="grouped", bufs=2))
-        quantised = ctx.enter_context(tc.tile_pool(name="quantised", bufs=2))
+        grouped = ctx.enter_context(tc.tile_pool(name="grouped", bufs=3))
+        quantised = ctx.enter_context(tc.tile_pool(name="quantised", bufs=3))
         results = ctx.enter_context(tc.tile_pool(name="results", bufs=4 * PACK))
-        psum = ctx.enter_context(tc.psum_pool(name="psum", bufs=PSUM_BANKS))
+        psum = ctx.enter_context(tc.psum_pool(name="psum", bufs=1))
+
+        def bank(kind, shape):
+            return psum.tile(shape, F32, tag=kind, name=kind + "_ps", bufs=BANKS[kind])
 
         def load_rows(pool, matrix, name):
             rows_sb = pool.tile([P, PACK * N], BF16, tag=name, name=name)
@@ -45,17 +43,27 @@ def tile_dualcrossmodalattention_pb_t_kernel(tc, x, Wv1, bv1, att2, gamma2, y, o
             return rows_sb
 
         x_in, att_in, y_in = {}, {}, {}
-        w_sb = load_rows(const, Wv1, "w_sb")
-        x_in[0] = load_rows(inputs, x[0], "x_sb")
+        def load_half(rows_sb, matrix, h):
+            nc.sync.dma_start(
+                out=rows_sb[:, h * 2 * N : (h + 1) * 2 * N],
+                in_=matrix.rearrange("(p h j) c -> p h (j c)", h=2, j=2)[:, h, :],
+            )
+
+        w_sb = const.tile([P, PACK * N], BF16)
+        x_in[0] = inputs.tile([P, PACK * N], BF16, tag="x_sb", name="x_sb")
+        load_half(w_sb, Wv1, 0)
         small = const.tile([P, N + GAMMA_COLS], BF16)
         nc.vector.memset(small[:], 0.0)
         nc.sync.dma_start(out=small[0:1, 0:N], in_=bv1.rearrange("(o d) -> o d", o=1))
         nc.sync.dma_start(out=small[0:1, N : N + 1], in_=gamma2.rearrange("(o g) -> o g", o=1))
-        for i in range(1 - TRANSPOSE_AHEAD, B):
-            if i + TRANSPOSE_AHEAD < B:
-                x_in[i + TRANSPOSE_AHEAD] = load_rows(inputs, x[i + TRANSPOSE_AHEAD], "x_sb")
-            if 0 <= i + PROJECT_AHEAD < B:
-                att_in[i + PROJECT_AHEAD] = load_rows(inputs, att2[i + PROJECT_AHEAD], "att_sb")
+        load_half(x_in[0], x[0], 0)
+        load_half(x_in[0], x[0], 1)
+        load_half(w_sb, Wv1, 1)
+        for i in range(-3, B):
+            if 0 <= i + 3 < B:
+                att_in[i + 3] = load_rows(inputs, att2[i + 3], "att_sb")
+            if i + 4 < B:
+                x_in[i + 4] = load_rows(inputs, x[i + 4], "x_sb")
             if 0 <= i:
                 y_in[i] = load_rows(inputs, y[i], "y_sb")
 
@@ -64,11 +72,22 @@ def tile_dualcrossmodalattention_pb_t_kernel(tc, x, Wv1, bv1, att2, gamma2, y, o
         ones = const.tile([P, P], BF16)
         nc.vector.memset(ones[:], 1.0)
 
-        def quantise(pool, name, values):
+        def quantised_tiles(pool, name):
             codes = pool.tile([P, N], U32, tag=name + "_codes", name=name + "_codes", align_bytes=64)
             scales = pool.tile([P, N], U8, tag=name + "_scales", name=name + "_scales", align_bytes=64)
-            nc.vector.quantize_mx(out=codes[:].bitcast(FP8X4), scales=scales[:], in_=values[:])
             return codes, scales
+
+        def quantise_columns(operand, values, first, end):
+            nc.vector.quantize_mx(
+                out=operand[0][:, first:end].bitcast(FP8X4),
+                scales=operand[1][:, first:end],
+                in_=values[:, PACK * first : PACK * end],
+            )
+
+        def quantise(pool, name, values):
+            operand = quantised_tiles(pool, name)
+            quantise_columns(operand, values, 0, N)
+            return operand
 
         def mx_pass(acc, stationary, s_cols, moving, m_cols):
             nc.tensor.matmul_mx(
@@ -81,38 +100,54 @@ def tile_dualcrossmodalattention_pb_t_kernel(tc, x, Wv1, bv1, att2, gamma2, y, o
                 stop=True,
             )
 
-        def transpose_words(rows_sb):
+        def transpose_half(rows_sb, h, kind):
             words = rows_sb[:].bitcast(F32)
-            flips = []
-            for first_group in (0, 2):
-                flip = psum.tile([P, PAIR, 2 * P], F32, tag="bank")
-                for jj in range(2):
-                    for u in range(PAIR):
-                        first = (first_group + jj) * (N // PAIR) + u * P
-                        nc.tensor.transpose(
-                            flip[:, u, jj * P : (jj + 1) * P], words[:, first : first + P], ident[:]
-                        )
-                flips.append(flip)
-            return flips
+            flip = bank(kind, [P, PAIR, 2 * P])
+            for jj in range(2):
+                for u in range(PAIR):
+                    first = (2 * h + jj) * (N // PAIR) + u * P
+                    nc.tensor.transpose(
+                        flip[:, u, jj * P : (jj + 1) * P], words[:, first : first + P], ident[:]
+                    )
+            return flip
 
-        def interleave_halves(pool, name, flips, copy):
-            values = pool.tile([P, PACK * N], BF16, tag=name, name=name, align_bytes=64)
+        def values_tile(pool, name):
+            return pool.tile([P, PACK * N], BF16, tag=name, name=name, align_bytes=64)
+
+        def interleave_half(values, flip, h, copy):
             value_words = values[:].bitcast(F32).rearrange("q (c u) -> q c u", u=PAIR)
+            copy(
+                out=value_words[:, h * 2 * P : (h + 1) * 2 * P, :],
+                in_=flip[:].rearrange("q u c -> q c u"),
+            )
+
+        def transpose_x(b, kind="flip"):
+            x_flips[b] = [transpose_half(x_in[b], h, kind) for h in range(2)]
+
+        def copy_x(b):
+            x_values[b] = values_tile(grouped, "x_values")
             for h in range(2):
-                copy(
-                    out=value_words[:, h * 2 * P : (h + 1) * 2 * P, :],
-                    in_=flips[h][:].rearrange("q u c -> q c u"),
-                )
-            return values
+                interleave_half(x_values[b], x_flips[b][h], h, nc.scalar.copy)
 
-        w_values = interleave_halves(const, "w_values", transpose_words(w_sb), nc.vector.tensor_copy)
-        w_mx = quantise(const, "w", w_values)
-        x_flips = {0: transpose_words(x_in[0])}
+        def quantise_x(b):
+            x_mx[b] = quantise(quantised, "x", x_values[b])
 
-        bias_ps = psum.tile([P, N], F32, tag="bank")
+        x_flips, x_values, att_values, v_banks, v_values, o_banks = {}, {}, {}, {}, {}, {}
+        x_mx, att_mx, v_mx = {}, {}, {}
+
+        w_values = values_tile(const, "w_values")
+        w_mx = quantised_tiles(const, "w")
+        w_flip = transpose_half(w_sb, 0, "v")
+        interleave_half(w_values, w_flip, 0, nc.vector.tensor_copy)
+        quantise_columns(w_mx, w_values, 0, N // 2)
+        transpose_x(0)
+        copy_x(0)
+        bias_ps = bank("o", [P, N])
         nc.tensor.matmul(out=bias_ps[:], lhsT=ones[:], rhs=small[:, 0:N], start=True, stop=True)
-        gamma_ps = psum.tile([P, GAMMA_COLS], F32, tag="bank")
+        gamma_ps = bank("o", [P, GAMMA_COLS])
         nc.tensor.matmul(out=gamma_ps[:], lhsT=ones[:], rhs=small[:, N:], start=True, stop=True)
+        x_mx[0] = quantised_tiles(quantised, "x")
+        quantise_columns(x_mx[0], x_values[0], 0, N // 2)
         bias_bc = const.tile([P, N], F32)
         nc.vector.tensor_copy(
             out=bias_bc[:].rearrange("q (j p) -> q j p", j=PACK),
@@ -120,9 +155,10 @@ def tile_dualcrossmodalattention_pb_t_kernel(tc, x, Wv1, bv1, att2, gamma2, y, o
         )
         gamma_bc = const.tile([P, 1], F32)
         nc.vector.tensor_copy(out=gamma_bc[:], in_=gamma_ps[:, 0:1])
-
-        x_values, att_values, v_banks, v_values = {}, {}, {}, {}
-        x_mx, att_mx, v_mx = {}, {}, {}
+        quantise_columns(x_mx[0], x_values[0], N // 2, N)
+        w_flip2 = transpose_half(w_sb, 1, "v")
+        interleave_half(w_values, w_flip2, 1, nc.vector.tensor_copy)
+        quantise_columns(w_mx, w_values, N // 2, N)
 
         def regroup_att(b):
             att_values[b] = grouped.tile([P, PACK * N], BF16, tag="att_values", name="att_values", align_bytes=64)
@@ -134,11 +170,11 @@ def tile_dualcrossmodalattention_pb_t_kernel(tc, x, Wv1, bv1, att2, gamma2, y, o
         def project(b):
             banks = []
             for i in range(PACK):
-                v_ps = psum.tile([P, PACK, P], F32, tag="bank")
+                v_ps = bank("v", [P, PACK, P])
                 for t in range(PACK):
                     mx_pass(v_ps[:, t, :], x_mx[b], slice(t * P, (t + 1) * P), w_mx, slice(i * P, (i + 1) * P))
                 banks.append(v_ps)
-            return banks
+            v_banks[b] = banks
 
         def add_bias(b):
             v_values[b] = grouped.tile([P, PACK * N], BF16, tag="v_values", name="v_values", align_bytes=64)
@@ -150,11 +186,14 @@ def tile_dualcrossmodalattention_pb_t_kernel(tc, x, Wv1, bv1, att2, gamma2, y, o
                     op=ADD,
                 )
 
-        def attend(b, c, on_vector):
-            o_ps = psum.tile([P, N], F32, tag="bank")
-            mx_pass(o_ps[:], v_mx[b], slice(c * P, (c + 1) * P), att_mx[b], slice(0, N))
+        def multiply(b, c, kind):
+            o_banks[b, c] = bank(kind, [P, N])
+            mx_pass(o_banks[b, c][:], v_mx[b], slice(c * P, (c + 1) * P), att_mx[b], slice(0, N))
+
+        def finish(b, c, on_vector):
+            o_ps = o_banks[b, c]
             y_rows = y_in[b][:, c * N : (c + 1) * N]
-            res = results.tile([P, N], F32)
+            res = results.tile([P, N], F32, tag="res", name="res")
             if on_vector:
                 nc.vector.scalar_tensor_tensor(
                     out=res[:], in0=o_ps[:], scalar=gamma_bc[:, 0:1], in1=y_rows, op0=MULT, op1=ADD
@@ -164,29 +203,60 @@ def tile_dualcrossmodalattention_pb_t_kernel(tc, x, Wv1, bv1, att2, gamma2, y, o
                 nc.gpsimd.tensor_tensor(out=res[:], in0=res[:], in1=y_rows, op=ADD)
             nc.sync.dma_start(out=out[b].rearrange("(p c) m -> p c m", c=PACK)[:, c, :], in_=res[:])
 
-        for i in range(1 - TRANSPOSE_AHEAD, B):
-            finishing = 0 <= i
-            if finishing:
-                att_mx[i] = quantise(quantised, "att", att_values[i])
-                v_mx[i] = quantise(quantised, "v", v_values[i])
-            if 0 <= i + PROJECT_AHEAD < B:
-                x_mx[i + PROJECT_AHEAD] = quantise(quantised, "x", x_values[i + PROJECT_AHEAD])
-            if finishing:
-                handed_over = 2 if i + BIAS_AHEAD < B else 1
-                for c in range(handed_over):
-                    attend(i, c, False)
-            if 0 <= i + BIAS_AHEAD < B:
-                add_bias(i + BIAS_AHEAD)
-            if finishing:
-                for c in range(handed_over, PACK):
-                    attend(i, c, True)
-            if 0 <= i + PROJECT_AHEAD < B:
-                v_banks[i + PROJECT_AHEAD] = project(i + PROJECT_AHEAD)
-            if 0 <= i + COPY_AHEAD < B:
-                x_values[i + COPY_AHEAD] = interleave_halves(
-                    grouped, "x_values", x_flips[i + COPY_AHEAD], nc.scalar.copy
-                )
-            if i + TRANSPOSE_AHEAD < B:
-                x_flips[i + TRANSPOSE_AHEAD] = transpose_words(x_in[i + TRANSPOSE_AHEAD])
-            if 0 <= i + PROJECT_AHEAD < B:
-                regroup_att(i + PROJECT_AHEAD)
+        def quantise_att(b):
+            att_mx[b] = quantise(quantised, "att", att_values[b])
+
+        def quantise_v(b):
+            v_mx[b] = quantise(quantised, "v", v_values[b])
+
+        project(0)
+        regroup_att(0)
+        transpose_x(1)
+        copy_x(1)
+        add_bias(0)
+        transpose_x(2, "o")
+        copy_x(2)
+        quantise_att(0)
+        quantise_x(1)
+        project(1)
+        quantise_v(0)
+        regroup_att(1)
+        quantise_x(2)
+        add_bias(1)
+        transpose_x(3)
+        project(2)
+        for i in range(1, B - 1):
+            if i + 2 < B:
+                copy_x(i + 2)
+            else:
+                regroup_att(i + 1)
+            quantise_att(i)
+            quantise_v(i)
+            if i + 2 < B:
+                quantise_x(i + 2)
+            for c in (0, 1):
+                multiply(i - 1, c, "o")
+                finish(i - 1, c, False)
+            if i + 3 < B:
+                transpose_x(i + 3)
+            for c in (2, 3):
+                multiply(i - 1, c, "o")
+            add_bias(i + 1)
+            for c in (2, 3):
+                finish(i - 1, c, True)
+            if i + 2 < B:
+                project(i + 2)
+                regroup_att(i + 1)
+        for c in range(PACK):
+            multiply(B - 2, c, "v")
+        for c in (0, 1):
+            finish(B - 2, c, False)
+        quantise_att(B - 1)
+        quantise_v(B - 1)
+        for c in range(PACK):
+            multiply(B - 1, c, "flip" if c < 2 else "o")
+        finish(B - 1, 0, False)
+        for c in (2, 3):
+            finish(B - 2, c, True)
+        for c in (1, 2, 3):
+            finish(B - 1, c, True)

@@ -20,6 +20,8 @@ PAIR = 2
 BANKS = {"flip": 2, "v": 4, "o": 2}
 GAMMA_COLS = 64
 
+WARM_UPS = 4
+
 FLOPS = 2 * B * (N * N * N + N * N * N)
 
 
@@ -29,7 +31,7 @@ def tile_dualcrossmodalattention_pb_t_kernel(tc, x, Wv1, bv1, att2, gamma2, y, o
         ctx.enter_context(tc.manual_schedule())
         const = ctx.enter_context(tc.tile_pool(name="const", bufs=1))
         inputs = ctx.enter_context(tc.tile_pool(name="inputs", bufs=B))
-        grouped = ctx.enter_context(tc.tile_pool(name="grouped", bufs=3))
+        grouped = ctx.enter_context(tc.tile_pool(name="grouped", bufs=4))
         quantised = ctx.enter_context(tc.tile_pool(name="quantised", bufs=3))
         results = ctx.enter_context(tc.tile_pool(name="results", bufs=4 * PACK))
         psum = ctx.enter_context(tc.psum_pool(name="psum", bufs=1))
@@ -52,6 +54,8 @@ def tile_dualcrossmodalattention_pb_t_kernel(tc, x, Wv1, bv1, att2, gamma2, y, o
         w_sb = const.tile([P, PACK * N], BF16)
         x_in[0] = inputs.tile([P, PACK * N], BF16, tag="x_sb", name="x_sb")
         load_half(w_sb, Wv1, 0)
+        ones = const.tile([P, P], BF16)
+        nc.vector.memset(ones[:], 1.0)
         small = const.tile([P, N + GAMMA_COLS], BF16)
         nc.vector.memset(small[:], 0.0)
         nc.sync.dma_start(out=small[0:1, 0:N], in_=bv1.rearrange("(o d) -> o d", o=1))
@@ -59,18 +63,21 @@ def tile_dualcrossmodalattention_pb_t_kernel(tc, x, Wv1, bv1, att2, gamma2, y, o
         load_half(x_in[0], x[0], 0)
         load_half(x_in[0], x[0], 1)
         load_half(w_sb, Wv1, 1)
-        for i in range(-3, B):
-            if 0 <= i + 3 < B:
-                att_in[i + 3] = load_rows(inputs, att2[i + 3], "att_sb")
-            if i + 4 < B:
-                x_in[i + 4] = load_rows(inputs, x[i + 4], "x_sb")
+        for i in range(-4, B):
+            if 1 <= i + 5 < B:
+                x_in[i + 5] = load_rows(inputs, x[i + 5], "x_sb")
+            if 0 <= i + 4 < B:
+                att_in[i + 4] = load_rows(inputs, att2[i + 4], "att_sb")
             if 0 <= i:
                 y_in[i] = load_rows(inputs, y[i], "y_sb")
 
         ident = const.tile([P, P], F32)
         make_identity(nc, ident[:])
-        ones = const.tile([P, P], BF16)
-        nc.vector.memset(ones[:], 1.0)
+        idle_ps = bank("v", [P, N])
+        for k in range(WARM_UPS):
+            nc.tensor.matmul(
+                out=idle_ps[:], lhsT=ones[:], rhs=ones[:, 0:1].to_broadcast([P, N]), start=True, stop=True
+            )
 
         def quantised_tiles(pool, name):
             codes = pool.tile([P, N], U32, tag=name + "_codes", name=name + "_codes", align_bytes=64)
@@ -133,6 +140,7 @@ def tile_dualcrossmodalattention_pb_t_kernel(tc, x, Wv1, bv1, att2, gamma2, y, o
             x_mx[b] = quantise(quantised, "x", x_values[b])
 
         x_flips, x_values, att_values, v_banks, v_values, o_banks = {}, {}, {}, {}, {}, {}
+        res_rows = {}
         x_mx, att_mx, v_mx = {}, {}, {}
 
         w_values = values_tile(const, "w_values")
@@ -161,7 +169,7 @@ def tile_dualcrossmodalattention_pb_t_kernel(tc, x, Wv1, bv1, att2, gamma2, y, o
         quantise_columns(w_mx, w_values, N // 2, N)
 
         def regroup_att(b):
-            att_values[b] = grouped.tile([P, PACK * N], BF16, tag="att_values", name="att_values", align_bytes=64)
+            att_values[b] = values_tile(grouped, "att_values")
             nc.scalar.copy(
                 out=att_values[b][:].rearrange("p (c i j) -> p c j i", i=4, j=PACK),
                 in_=att_in[b][:].rearrange("p (j c i) -> p c j i", j=PACK, i=4),
@@ -194,6 +202,7 @@ def tile_dualcrossmodalattention_pb_t_kernel(tc, x, Wv1, bv1, att2, gamma2, y, o
             o_ps = o_banks[b, c]
             y_rows = y_in[b][:, c * N : (c + 1) * N]
             res = results.tile([P, N], F32, tag="res", name="res")
+            res_rows[b, c] = res
             if on_vector:
                 nc.vector.scalar_tensor_tensor(
                     out=res[:], in0=o_ps[:], scalar=gamma_bc[:, 0:1], in1=y_rows, op0=MULT, op1=ADD
@@ -201,7 +210,9 @@ def tile_dualcrossmodalattention_pb_t_kernel(tc, x, Wv1, bv1, att2, gamma2, y, o
             else:
                 nc.scalar.activation(out=res[:], in_=o_ps[:], func=COPY, scale=gamma_bc[:, 0:1])
                 nc.gpsimd.tensor_tensor(out=res[:], in0=res[:], in1=y_rows, op=ADD)
-            nc.sync.dma_start(out=out[b].rearrange("(p c) m -> p c m", c=PACK)[:, c, :], in_=res[:])
+
+        def store(b, c):
+            nc.sync.dma_start(out=out[b].rearrange("(p c) m -> p c m", c=PACK)[:, c, :], in_=res_rows[b, c][:])
 
         def quantise_att(b):
             att_mx[b] = quantise(quantised, "att", att_values[b])
@@ -216,20 +227,20 @@ def tile_dualcrossmodalattention_pb_t_kernel(tc, x, Wv1, bv1, att2, gamma2, y, o
         add_bias(0)
         transpose_x(2, "o")
         copy_x(2)
+        regroup_att(1)
         quantise_att(0)
         quantise_x(1)
         project(1)
+        transpose_x(3)
         quantise_v(0)
-        regroup_att(1)
+        copy_x(3)
         quantise_x(2)
         add_bias(1)
-        transpose_x(3)
+        regroup_att(2)
+        transpose_x(4)
         project(2)
         for i in range(1, B - 1):
-            if i + 2 < B:
-                copy_x(i + 2)
-            else:
-                regroup_att(i + 1)
+            handed_over = 3 if i % 2 == 0 else 2
             quantise_att(i)
             quantise_v(i)
             if i + 2 < B:
@@ -238,25 +249,33 @@ def tile_dualcrossmodalattention_pb_t_kernel(tc, x, Wv1, bv1, att2, gamma2, y, o
                 multiply(i - 1, c, "o")
                 finish(i - 1, c, False)
             if i + 3 < B:
-                transpose_x(i + 3)
+                copy_x(i + 3)
             for c in (2, 3):
                 multiply(i - 1, c, "o")
+                if c < handed_over:
+                    finish(i - 1, c, False)
             add_bias(i + 1)
-            for c in (2, 3):
+            for c in range(handed_over, PACK):
                 finish(i - 1, c, True)
+            for c in range(PACK):
+                store(i - 1, c)
             if i + 2 < B:
                 project(i + 2)
-                regroup_att(i + 1)
+                regroup_att(i + 2)
+            if i + 4 < B:
+                transpose_x(i + 4)
         for c in range(PACK):
             multiply(B - 2, c, "v")
-        for c in (0, 1):
-            finish(B - 2, c, False)
         quantise_att(B - 1)
         quantise_v(B - 1)
         for c in range(PACK):
             multiply(B - 1, c, "flip" if c < 2 else "o")
-        finish(B - 1, 0, False)
-        for c in (2, 3):
+        for c in (0, 1):
+            finish(B - 1, c, False)
+        for c in range(PACK):
             finish(B - 2, c, True)
-        for c in (1, 2, 3):
+            store(B - 2, c)
+        for c in (2, 3):
             finish(B - 1, c, True)
+        for c in (0, 2, 1, 3):
+            store(B - 1, c)

@@ -10,16 +10,15 @@ U8 = mybir.dt.uint8
 FP8X4 = mybir.dt.float8_e4m3fn_x4
 ADD = mybir.AluOpType.add
 MULT = mybir.AluOpType.mult
-COPY = mybir.ActivationFunctionType.Copy
+IDENTITY = mybir.ActivationFunctionType.Identity
 
 B = 8
 N = 512
 P = 128
 PACK = 4
 PAIR = 2
-BANKS = {"flip": 2, "v": 4, "o": 2}
 GAMMA_COLS = 64
-
+BANKS = {"x": 2, "v": 2, "vt": 2, "o": 2}
 WARM_UPS = 4
 
 FLOPS = 2 * B * (N * N * N + N * N * N)
@@ -31,7 +30,7 @@ def tile_dualcrossmodalattention_pb_t_kernel(tc, x, Wv1, bv1, att2, gamma2, y, o
         ctx.enter_context(tc.manual_schedule())
         const = ctx.enter_context(tc.tile_pool(name="const", bufs=1))
         inputs = ctx.enter_context(tc.tile_pool(name="inputs", bufs=B))
-        grouped = ctx.enter_context(tc.tile_pool(name="grouped", bufs=4))
+        work = ctx.enter_context(tc.tile_pool(name="work", bufs=3))
         quantised = ctx.enter_context(tc.tile_pool(name="quantised", bufs=3))
         results = ctx.enter_context(tc.tile_pool(name="results", bufs=4 * PACK))
         psum = ctx.enter_context(tc.psum_pool(name="psum", bufs=1))
@@ -39,45 +38,49 @@ def tile_dualcrossmodalattention_pb_t_kernel(tc, x, Wv1, bv1, att2, gamma2, y, o
         def bank(kind, shape):
             return psum.tile(shape, F32, tag=kind, name=kind + "_ps", bufs=BANKS[kind])
 
-        def load_rows(pool, matrix, name):
-            rows_sb = pool.tile([P, PACK * N], BF16, tag=name, name=name)
+        def load_rows(matrix, name):
+            rows_sb = inputs.tile([P, PACK * N], BF16, tag=name, name=name)
             nc.sync.dma_start(out=rows_sb[:], in_=matrix.rearrange("(p j) c -> p (j c)", j=PACK))
             return rows_sb
 
-        x_in, att_in, y_in = {}, {}, {}
         def load_half(rows_sb, matrix, h):
             nc.sync.dma_start(
                 out=rows_sb[:, h * 2 * N : (h + 1) * 2 * N],
                 in_=matrix.rearrange("(p h j) c -> p h (j c)", h=2, j=2)[:, h, :],
             )
 
+        x_in, att_in, y_in = {}, {}, {}
         w_sb = const.tile([P, PACK * N], BF16)
         x_in[0] = inputs.tile([P, PACK * N], BF16, tag="x_sb", name="x_sb")
         load_half(w_sb, Wv1, 0)
         ones = const.tile([P, P], BF16)
         nc.vector.memset(ones[:], 1.0)
-        small = const.tile([P, N + GAMMA_COLS], BF16)
+        small = const.tile([P, GAMMA_COLS], BF16)
         nc.vector.memset(small[:], 0.0)
-        nc.sync.dma_start(out=small[0:1, 0:N], in_=bv1.rearrange("(o d) -> o d", o=1))
-        nc.sync.dma_start(out=small[0:1, N : N + 1], in_=gamma2.rearrange("(o g) -> o g", o=1))
+        nc.sync.dma_start(out=small[0:1, 0:1], in_=gamma2.rearrange("(o g) -> o g", o=1))
         load_half(x_in[0], x[0], 0)
         load_half(x_in[0], x[0], 1)
         load_half(w_sb, Wv1, 1)
+        bias_sb = const.tile([P, PACK], BF16)
+        nc.sync.dma_start(out=bias_sb[:], in_=bv1.rearrange("(p j) -> p j", j=PACK))
         for i in range(-4, B):
             if 1 <= i + 5 < B:
-                x_in[i + 5] = load_rows(inputs, x[i + 5], "x_sb")
+                x_in[i + 5] = load_rows(x[i + 5], "x_sb")
             if 0 <= i + 4 < B:
-                att_in[i + 4] = load_rows(inputs, att2[i + 4], "att_sb")
-            if 0 <= i:
-                y_in[i] = load_rows(inputs, y[i], "y_sb")
+                att_in[i + 4] = load_rows(att2[i + 4], "att_sb")
+            if 0 <= i + 2 < B:
+                y_in[i + 2] = load_rows(y[i + 2], "y_sb")
 
         ident = const.tile([P, P], F32)
         make_identity(nc, ident[:])
-        idle_ps = bank("v", [P, N])
+        idle_ps = bank("o", [P, N])
         for k in range(WARM_UPS):
             nc.tensor.matmul(
                 out=idle_ps[:], lhsT=ones[:], rhs=ones[:, 0:1].to_broadcast([P, N]), start=True, stop=True
             )
+
+        def values_tile(pool, name):
+            return pool.tile([P, PACK * N], BF16, tag=name, name=name, align_bytes=64)
 
         def quantised_tiles(pool, name):
             codes = pool.tile([P, N], U32, tag=name + "_codes", name=name + "_codes", align_bytes=64)
@@ -91,18 +94,19 @@ def tile_dualcrossmodalattention_pb_t_kernel(tc, x, Wv1, bv1, att2, gamma2, y, o
                 in_=values[:, PACK * first : PACK * end],
             )
 
-        def quantise(pool, name, values):
-            operand = quantised_tiles(pool, name)
+        def quantise(name, values):
+            operand = quantised_tiles(quantised, name)
             quantise_columns(operand, values, 0, N)
             return operand
 
-        def mx_pass(acc, stationary, s_cols, moving, m_cols):
+        def mx_pass(acc, stationary, j, moving):
+            cols = slice(j * P, (j + 1) * P)
             nc.tensor.matmul_mx(
                 out=acc,
-                lhsT=stationary[0][:, s_cols].bitcast(FP8X4),
-                lhsT_scale=stationary[1][:, s_cols],
-                rhs=moving[0][:, m_cols].bitcast(FP8X4),
-                rhs_scale=moving[1][:, m_cols],
+                lhsT=stationary[0][:, cols].bitcast(FP8X4),
+                lhsT_scale=stationary[1][:, cols],
+                rhs=moving[0][:].bitcast(FP8X4),
+                rhs_scale=moving[1][:],
                 start=True,
                 stop=True,
             )
@@ -118,9 +122,6 @@ def tile_dualcrossmodalattention_pb_t_kernel(tc, x, Wv1, bv1, att2, gamma2, y, o
                     )
             return flip
 
-        def values_tile(pool, name):
-            return pool.tile([P, PACK * N], BF16, tag=name, name=name, align_bytes=64)
-
         def interleave_half(values, flip, h, copy):
             value_words = values[:].bitcast(F32).rearrange("q (c u) -> q c u", u=PAIR)
             copy(
@@ -128,154 +129,132 @@ def tile_dualcrossmodalattention_pb_t_kernel(tc, x, Wv1, bv1, att2, gamma2, y, o
                 in_=flip[:].rearrange("q u c -> q c u"),
             )
 
-        def transpose_x(b, kind="flip"):
-            x_flips[b] = [transpose_half(x_in[b], h, kind) for h in range(2)]
+        x_flips, x_values, v_rows, v_flips, v_values, att_values = {}, {}, {}, {}, {}, {}
+        x_mx, att_mx, v_mx, v_banks, o_banks = {}, {}, {}, {}, {}
 
-        def copy_x(b):
-            x_values[b] = values_tile(grouped, "x_values")
-            for h in range(2):
-                interleave_half(x_values[b], x_flips[b][h], h, nc.scalar.copy)
+        def transpose_x(b, h):
+            x_flips[b, h] = transpose_half(x_in[b], h, "x")
+
+        def copy_x(b, h):
+            if h == 0:
+                x_values[b] = values_tile(work, "x_values")
+            interleave_half(x_values[b], x_flips[b, h], h, nc.scalar.copy)
 
         def quantise_x(b):
-            x_mx[b] = quantise(quantised, "x", x_values[b])
+            x_mx[b] = quantise("x", x_values[b])
 
-        x_flips, x_values, att_values, v_banks, v_values, o_banks = {}, {}, {}, {}, {}, {}
-        res_rows = {}
-        x_mx, att_mx, v_mx = {}, {}, {}
+        def project(b, j):
+            v_banks[b, j] = bank("v", [P, N])
+            mx_pass(v_banks[b, j][:], w_mx, j, x_mx[b])
 
+        def add_bias(b, j):
+            if j == 0:
+                v_rows[b] = work.tile([P, PACK * N], BF16, tag="v_rows", name="v_rows")
+            nc.scalar.activation(
+                out=v_rows[b][:, j * N : (j + 1) * N].rearrange("p (u q e) -> p u q e", u=PAIR, e=PAIR),
+                in_=v_banks[b, j][:].rearrange("p (u e q) -> p u q e", u=PAIR, e=PAIR),
+                func=IDENTITY,
+                bias=bias_sb[:, j : j + 1],
+            )
+
+        def transpose_v(b, h):
+            v_flips[b, h] = transpose_half(v_rows[b], h, "vt")
+
+        def copy_v(b, h):
+            if h == 0:
+                v_values[b] = values_tile(work, "v_values")
+            interleave_half(v_values[b], v_flips[b, h], h, nc.scalar.copy)
+
+        def quantise_v(b):
+            v_mx[b] = quantise("v", v_values[b])
+
+        def regroup_att(b):
+            att_values[b] = att_pool.tile([P, PACK * N], BF16, tag="att_values", name="att_values", align_bytes=64)
+            for k in range(4):
+                cols = slice(k * P, (k + 1) * P)
+                nc.gpsimd.tensor_scalar(
+                    out=att_values[b][:].rearrange("p (c j) -> p c j", j=PACK)[:, cols, :],
+                    in0=att_in[b][:].rearrange("p (j c) -> p c j", j=PACK)[:, cols, :],
+                    scalar1=1.0,
+                    scalar2=0.0,
+                    op0=MULT,
+                    op1=ADD,
+                )
+
+        def quantise_att(b):
+            att_mx[b] = quantise("att", att_values[b])
+
+        def multiply(b, c):
+            o_banks[b, c] = bank("o", [P, N])
+            mx_pass(o_banks[b, c][:], v_mx[b], c, att_mx[b])
+
+        def finish(b, c):
+            res = results.tile([P, N], F32, tag="res", name="res")
+            nc.vector.scalar_tensor_tensor(
+                out=res[:],
+                in0=o_banks[b, c][:],
+                scalar=gamma_bc[:, 0:1],
+                in1=y_in[b][:, c * N : (c + 1) * N],
+                op0=MULT,
+                op1=ADD,
+            )
+            nc.sync.dma_start(out=out[b].rearrange("(p c) m -> p c m", c=PACK)[:, c, :], in_=res[:])
+
+        att_pool = ctx.enter_context(tc.tile_pool(name="att_pool", bufs=2))
         w_values = values_tile(const, "w_values")
         w_mx = quantised_tiles(const, "w")
-        w_flip = transpose_half(w_sb, 0, "v")
-        interleave_half(w_values, w_flip, 0, nc.vector.tensor_copy)
+        interleave_half(w_values, transpose_half(w_sb, 0, "o"), 0, nc.vector.tensor_copy)
         quantise_columns(w_mx, w_values, 0, N // 2)
-        transpose_x(0)
-        copy_x(0)
-        bias_ps = bank("o", [P, N])
-        nc.tensor.matmul(out=bias_ps[:], lhsT=ones[:], rhs=small[:, 0:N], start=True, stop=True)
-        gamma_ps = bank("o", [P, GAMMA_COLS])
-        nc.tensor.matmul(out=gamma_ps[:], lhsT=ones[:], rhs=small[:, N:], start=True, stop=True)
+        for h in range(2):
+            transpose_x(0, h)
+            copy_x(0, h)
+        gamma_ps = bank("vt", [P, GAMMA_COLS])
+        nc.tensor.matmul(out=gamma_ps[:], lhsT=ones[:], rhs=small[:], start=True, stop=True)
         x_mx[0] = quantised_tiles(quantised, "x")
         quantise_columns(x_mx[0], x_values[0], 0, N // 2)
-        bias_bc = const.tile([P, N], F32)
-        nc.vector.tensor_copy(
-            out=bias_bc[:].rearrange("q (j p) -> q j p", j=PACK),
-            in_=bias_ps[:].rearrange("q (p j) -> q j p", j=PACK),
-        )
         gamma_bc = const.tile([P, 1], F32)
         nc.vector.tensor_copy(out=gamma_bc[:], in_=gamma_ps[:, 0:1])
         quantise_columns(x_mx[0], x_values[0], N // 2, N)
-        w_flip2 = transpose_half(w_sb, 1, "v")
-        interleave_half(w_values, w_flip2, 1, nc.vector.tensor_copy)
+        interleave_half(w_values, transpose_half(w_sb, 1, "o"), 1, nc.vector.tensor_copy)
         quantise_columns(w_mx, w_values, N // 2, N)
 
-        def regroup_att(b):
-            att_values[b] = values_tile(grouped, "att_values")
-            nc.scalar.copy(
-                out=att_values[b][:].rearrange("p (c i j) -> p c j i", i=4, j=PACK),
-                in_=att_in[b][:].rearrange("p (j c i) -> p c j i", j=PACK, i=4),
-            )
+        def at(stage, b, *which):
+            if 0 <= b < B:
+                stage(b, *which)
 
-        def project(b):
-            banks = []
-            for i in range(PACK):
-                v_ps = bank("v", [P, PACK, P])
-                for t in range(PACK):
-                    mx_pass(v_ps[:, t, :], x_mx[b], slice(t * P, (t + 1) * P), w_mx, slice(i * P, (i + 1) * P))
-                banks.append(v_ps)
-            v_banks[b] = banks
+        def at_x(stage, b, *which):
+            if 1 <= b < B:
+                stage(b, *which)
 
-        def add_bias(b):
-            v_values[b] = grouped.tile([P, PACK * N], BF16, tag="v_values", name="v_values", align_bytes=64)
-            for i in range(PACK):
-                nc.vector.tensor_tensor(
-                    out=v_values[b][:, i * PACK * P : (i + 1) * PACK * P].rearrange("p (d t) -> p d t", t=PACK),
-                    in0=v_banks[b][i][:].rearrange("p t d -> p d t"),
-                    in1=bias_bc[:, i * P : (i + 1) * P].unsqueeze(2).to_broadcast([P, P, PACK]),
-                    op=ADD,
-                )
-
-        def multiply(b, c, kind):
-            o_banks[b, c] = bank(kind, [P, N])
-            mx_pass(o_banks[b, c][:], v_mx[b], slice(c * P, (c + 1) * P), att_mx[b], slice(0, N))
-
-        def finish(b, c, on_vector):
-            o_ps = o_banks[b, c]
-            y_rows = y_in[b][:, c * N : (c + 1) * N]
-            res = results.tile([P, N], F32, tag="res", name="res")
-            res_rows[b, c] = res
-            if on_vector:
-                nc.vector.scalar_tensor_tensor(
-                    out=res[:], in0=o_ps[:], scalar=gamma_bc[:, 0:1], in1=y_rows, op0=MULT, op1=ADD
-                )
-            else:
-                nc.scalar.activation(out=res[:], in_=o_ps[:], func=COPY, scale=gamma_bc[:, 0:1])
-                nc.gpsimd.tensor_tensor(out=res[:], in0=res[:], in1=y_rows, op=ADD)
-
-        def store(b, c):
-            nc.sync.dma_start(out=out[b].rearrange("(p c) m -> p c m", c=PACK)[:, c, :], in_=res_rows[b, c][:])
-
-        def quantise_att(b):
-            att_mx[b] = quantise(quantised, "att", att_values[b])
-
-        def quantise_v(b):
-            v_mx[b] = quantise(quantised, "v", v_values[b])
-
-        project(0)
         regroup_att(0)
-        transpose_x(1)
-        copy_x(1)
-        add_bias(0)
-        transpose_x(2, "o")
-        copy_x(2)
         regroup_att(1)
-        quantise_att(0)
-        quantise_x(1)
-        project(1)
-        transpose_x(3)
-        quantise_v(0)
-        copy_x(3)
-        quantise_x(2)
-        add_bias(1)
-        regroup_att(2)
-        transpose_x(4)
-        project(2)
-        for i in range(1, B - 1):
-            handed_over = 3 if i % 2 == 0 else 2
-            quantise_att(i)
-            quantise_v(i)
-            if i + 2 < B:
-                quantise_x(i + 2)
-            for c in (0, 1):
-                multiply(i - 1, c, "o")
-                finish(i - 1, c, False)
-            if i + 3 < B:
-                copy_x(i + 3)
-            for c in (2, 3):
-                multiply(i - 1, c, "o")
-                if c < handed_over:
-                    finish(i - 1, c, False)
-            add_bias(i + 1)
-            for c in range(handed_over, PACK):
-                finish(i - 1, c, True)
-            for c in range(PACK):
-                store(i - 1, c)
-            if i + 2 < B:
-                project(i + 2)
-                regroup_att(i + 2)
-            if i + 4 < B:
-                transpose_x(i + 4)
-        for c in range(PACK):
-            multiply(B - 2, c, "v")
-        quantise_att(B - 1)
-        quantise_v(B - 1)
-        for c in range(PACK):
-            multiply(B - 1, c, "flip" if c < 2 else "o")
-        for c in (0, 1):
-            finish(B - 1, c, False)
-        for c in range(PACK):
-            finish(B - 2, c, True)
-            store(B - 2, c)
-        for c in (2, 3):
-            finish(B - 1, c, True)
-        for c in (0, 2, 1, 3):
-            store(B - 1, c)
+        for i in range(-2, B + 1):
+            at(quantise_v, i)
+            at(add_bias, i + 1, 0)
+            at_x(transpose_x, i + 3, 0)
+            at(finish, i - 1, 3)
+            at(project, i + 1, 2)
+            at(multiply, i, 0)
+            at_x(quantise_x, i + 2)
+            at(add_bias, i + 1, 1)
+            at(project, i + 1, 3)
+            at(multiply, i, 1)
+            at_x(copy_x, i + 3, 0)
+            at_x(transpose_x, i + 3, 1)
+            at(finish, i, 0)
+            at(add_bias, i + 1, 2)
+            at(add_bias, i + 1, 3)
+            at(quantise_att, i + 1)
+            if i + 1 >= 0:
+                at(regroup_att, i + 3)
+            at(transpose_v, i + 1, 0)
+            at(transpose_v, i + 1, 1)
+            at(project, i + 2, 0)
+            at(finish, i, 1)
+            at(multiply, i, 2)
+            at(project, i + 2, 1)
+            at(multiply, i, 3)
+            at_x(copy_x, i + 3, 1)
+            at(copy_v, i + 1, 0)
+            at(copy_v, i + 1, 1)
+            at(finish, i, 2)

@@ -20,6 +20,8 @@ PAIR = 2
 GAMMA_COLS = 64
 BANKS = {"x": 2, "v": 2, "vt": 2, "o": 2}
 WARM_UPS = 4
+GPSIMD_COLS = 320
+FINE_STORES = 2
 
 FLOPS = 2 * B * (N * N * N + N * N * N)
 
@@ -32,7 +34,7 @@ def tile_dualcrossmodalattention_pb_t_kernel(tc, x, Wv1, bv1, att2, gamma2, y, o
         inputs = ctx.enter_context(tc.tile_pool(name="inputs", bufs=B))
         work = ctx.enter_context(tc.tile_pool(name="work", bufs=3))
         quantised = ctx.enter_context(tc.tile_pool(name="quantised", bufs=3))
-        results = ctx.enter_context(tc.tile_pool(name="results", bufs=4 * PACK))
+        results = ctx.enter_context(tc.tile_pool(name="results", bufs=10))
         psum = ctx.enter_context(tc.psum_pool(name="psum", bufs=1))
 
         def bank(kind, shape):
@@ -130,7 +132,7 @@ def tile_dualcrossmodalattention_pb_t_kernel(tc, x, Wv1, bv1, att2, gamma2, y, o
             )
 
         x_flips, x_values, v_rows, v_flips, v_values, att_values = {}, {}, {}, {}, {}, {}
-        x_mx, att_mx, v_mx, v_banks, o_banks = {}, {}, {}, {}, {}
+        x_mx, att_mx, v_mx, v_banks, o_banks, results_of = {}, {}, {}, {}, {}, {}
 
         def transpose_x(b, h):
             x_flips[b, h] = transpose_half(x_in[b], h, "x")
@@ -168,18 +170,24 @@ def tile_dualcrossmodalattention_pb_t_kernel(tc, x, Wv1, bv1, att2, gamma2, y, o
         def quantise_v(b):
             v_mx[b] = quantise("v", v_values[b])
 
-        def regroup_att(b):
-            att_values[b] = att_pool.tile([P, PACK * N], BF16, tag="att_values", name="att_values", align_bytes=64)
-            for k in range(4):
-                cols = slice(k * P, (k + 1) * P)
-                nc.gpsimd.tensor_scalar(
-                    out=att_values[b][:].rearrange("p (c j) -> p c j", j=PACK)[:, cols, :],
-                    in0=att_in[b][:].rearrange("p (j c) -> p c j", j=PACK)[:, cols, :],
-                    scalar1=1.0,
-                    scalar2=0.0,
-                    op0=MULT,
-                    op1=ADD,
+        def regroup_att(b, first, end, copy):
+            if b not in att_values:
+                att_values[b] = att_pool.tile(
+                    [P, PACK * N], BF16, tag="att_values", name="att_values", align_bytes=64
                 )
+            copy(
+                out=att_values[b][:].rearrange("p (c j) -> p c j", j=PACK)[:, first:end, :],
+                in_=att_in[b][:].rearrange("p (j c) -> p c j", j=PACK)[:, first:end, :],
+            )
+
+        def gpsimd_copy(out, in_):
+            nc.gpsimd.tensor_scalar(out=out, in0=in_, scalar1=1.0, scalar2=0.0, op0=MULT, op1=ADD)
+
+        def regroup_gpsimd(b):
+            regroup_att(b, 0, GPSIMD_COLS, gpsimd_copy)
+
+        def regroup_vector(b):
+            regroup_att(b, GPSIMD_COLS, N, nc.vector.tensor_copy)
 
         def quantise_att(b):
             att_mx[b] = quantise("att", att_values[b])
@@ -189,16 +197,22 @@ def tile_dualcrossmodalattention_pb_t_kernel(tc, x, Wv1, bv1, att2, gamma2, y, o
             mx_pass(o_banks[b, c][:], v_mx[b], c, att_mx[b])
 
         def finish(b, c):
-            res = results.tile([P, N], F32, tag="res", name="res")
+            if c % 2 == 0:
+                results_of[b] = results.tile([P, 2, N], F32, tag="res", name="res")
+            res = results_of[b]
             nc.vector.scalar_tensor_tensor(
-                out=res[:],
+                out=res[:, c % 2, :],
                 in0=o_banks[b, c][:],
                 scalar=gamma_bc[:, 0:1],
                 in1=y_in[b][:, c * N : (c + 1) * N],
                 op0=MULT,
                 op1=ADD,
             )
-            nc.sync.dma_start(out=out[b].rearrange("(p c) m -> p c m", c=PACK)[:, c, :], in_=res[:])
+            rows = out[b].rearrange("(p c) m -> p c m", c=PACK)
+            if b >= B - FINE_STORES:
+                nc.sync.dma_start(out=rows[:, c, :], in_=res[:, c % 2, :])
+            elif c % 2 == 1:
+                nc.sync.dma_start(out=rows[:, c - 1 : c + 1, :], in_=res[:])
 
         att_pool = ctx.enter_context(tc.tile_pool(name="att_pool", bufs=2))
         w_values = values_tile(const, "w_values")
@@ -226,35 +240,34 @@ def tile_dualcrossmodalattention_pb_t_kernel(tc, x, Wv1, bv1, att2, gamma2, y, o
             if 1 <= b < B:
                 stage(b, *which)
 
-        regroup_att(0)
-        regroup_att(1)
+        regroup_gpsimd(0)
         for i in range(-2, B + 1):
-            at(quantise_v, i)
+            at(project, i + 1, 0)
+            at(project, i + 1, 1)
+            at(multiply, i - 1, 2)
+            at(multiply, i - 1, 3)
+            at(finish, i - 1, 2)
             at(add_bias, i + 1, 0)
-            at_x(transpose_x, i + 3, 0)
-            at(finish, i - 1, 3)
-            at(project, i + 1, 2)
-            at(multiply, i, 0)
-            at_x(quantise_x, i + 2)
             at(add_bias, i + 1, 1)
-            at(project, i + 1, 3)
-            at(multiply, i, 1)
+            at_x(transpose_x, i + 3, 0)
             at_x(copy_x, i + 3, 0)
-            at_x(transpose_x, i + 3, 1)
-            at(finish, i, 0)
+            at(project, i + 1, 2)
+            at(project, i + 1, 3)
             at(add_bias, i + 1, 2)
             at(add_bias, i + 1, 3)
-            at(quantise_att, i + 1)
-            if i + 1 >= 0:
-                at(regroup_att, i + 3)
+            at_x(transpose_x, i + 3, 1)
+            at_x(copy_x, i + 3, 1)
+            at(quantise_v, i)
+            at(regroup_vector, i + 2)
+            at(finish, i - 1, 3)
+            at(multiply, i, 0)
+            at(multiply, i, 1)
             at(transpose_v, i + 1, 0)
             at(transpose_v, i + 1, 1)
-            at(project, i + 2, 0)
-            at(finish, i, 1)
-            at(multiply, i, 2)
-            at(project, i + 2, 1)
-            at(multiply, i, 3)
-            at_x(copy_x, i + 3, 1)
             at(copy_v, i + 1, 0)
             at(copy_v, i + 1, 1)
-            at(finish, i, 2)
+            at_x(quantise_x, i + 2)
+            at(quantise_att, i + 1)
+            at(regroup_gpsimd, i + 3)
+            at(finish, i, 0)
+            at(finish, i, 1)

@@ -18,10 +18,11 @@ P = 128
 PACK = 4
 PAIR = 2
 GAMMA_COLS = 64
-BANKS = {"x": 2, "v": 2, "vt": 2, "o": 2}
+BANKS = {"x": 2, "v": 2, "vt": 1, "o": 3}
 WARM_UPS = 4
-GPSIMD_COLS = 320
-FINE_STORES = 2
+VECTOR_SAMPLES = 2
+GPSIMD_COLS = 384
+FINE_STORES = 3
 
 FLOPS = 2 * B * (N * N * N + N * N * N)
 
@@ -140,7 +141,8 @@ def tile_dualcrossmodalattention_pb_t_kernel(tc, x, Wv1, bv1, att2, gamma2, y, o
         def copy_x(b, h):
             if h == 0:
                 x_values[b] = values_tile(work, "x_values")
-            interleave_half(x_values[b], x_flips[b, h], h, nc.scalar.copy)
+            copy = nc.vector.tensor_copy if (b, h) == (2, 1) else nc.scalar.copy
+            interleave_half(x_values[b], x_flips[b, h], h, copy)
 
         def quantise_x(b):
             x_mx[b] = quantise("x", x_values[b])
@@ -184,10 +186,11 @@ def tile_dualcrossmodalattention_pb_t_kernel(tc, x, Wv1, bv1, att2, gamma2, y, o
             nc.gpsimd.tensor_scalar(out=out, in0=in_, scalar1=1.0, scalar2=0.0, op0=MULT, op1=ADD)
 
         def regroup_gpsimd(b):
-            regroup_att(b, 0, GPSIMD_COLS, gpsimd_copy)
+            if b >= VECTOR_SAMPLES:
+                regroup_att(b, 0, GPSIMD_COLS, gpsimd_copy)
 
         def regroup_vector(b):
-            regroup_att(b, GPSIMD_COLS, N, nc.vector.tensor_copy)
+            regroup_att(b, GPSIMD_COLS if b >= VECTOR_SAMPLES else 0, N, nc.vector.tensor_copy)
 
         def quantise_att(b):
             att_mx[b] = quantise("att", att_values[b])
@@ -196,23 +199,26 @@ def tile_dualcrossmodalattention_pb_t_kernel(tc, x, Wv1, bv1, att2, gamma2, y, o
             o_banks[b, c] = bank("o", [P, N])
             mx_pass(o_banks[b, c][:], v_mx[b], c, att_mx[b])
 
-        def finish(b, c):
+        def store(b, first, end):
+            rows = out[b].rearrange("(p c) m -> p c m", c=PACK)[:, first:end, :]
+            pair = first // 2
+            nc.sync.dma_start(out=rows, in_=results_of[b, pair][:, first - 2 * pair : end - 2 * pair, :])
+
+        def result_rows(b, c):
             if c % 2 == 0:
-                results_of[b] = results.tile([P, 2, N], F32, tag="res", name="res")
-            res = results_of[b]
+                results_of[b, c // 2] = results.tile([P, 2, N], F32, tag="res", name="res")
+            return results_of[b, c // 2][:, c % 2, :]
+
+        def finish(b, c):
+            res = result_rows(b, c)
+            y_rows = y_in[b][:, c * N : (c + 1) * N]
             nc.vector.scalar_tensor_tensor(
-                out=res[:, c % 2, :],
-                in0=o_banks[b, c][:],
-                scalar=gamma_bc[:, 0:1],
-                in1=y_in[b][:, c * N : (c + 1) * N],
-                op0=MULT,
-                op1=ADD,
+                out=res, in0=o_banks[b, c][:], scalar=gamma_bc[:, 0:1], in1=y_rows, op0=MULT, op1=ADD
             )
-            rows = out[b].rearrange("(p c) m -> p c m", c=PACK)
             if b >= B - FINE_STORES:
-                nc.sync.dma_start(out=rows[:, c, :], in_=res[:, c % 2, :])
+                store(b, c, c + 1)
             elif c % 2 == 1:
-                nc.sync.dma_start(out=rows[:, c - 1 : c + 1, :], in_=res[:])
+                store(b, c - 1, c + 1)
 
         att_pool = ctx.enter_context(tc.tile_pool(name="att_pool", bufs=2))
         w_values = values_tile(const, "w_values")
@@ -240,34 +246,33 @@ def tile_dualcrossmodalattention_pb_t_kernel(tc, x, Wv1, bv1, att2, gamma2, y, o
             if 1 <= b < B:
                 stage(b, *which)
 
-        regroup_gpsimd(0)
-        for i in range(-2, B + 1):
-            at(project, i + 1, 0)
-            at(project, i + 1, 1)
-            at(multiply, i - 1, 2)
-            at(multiply, i - 1, 3)
-            at(finish, i - 1, 2)
-            at(add_bias, i + 1, 0)
-            at(add_bias, i + 1, 1)
-            at_x(transpose_x, i + 3, 0)
-            at_x(copy_x, i + 3, 0)
-            at(project, i + 1, 2)
-            at(project, i + 1, 3)
-            at(add_bias, i + 1, 2)
-            at(add_bias, i + 1, 3)
-            at_x(transpose_x, i + 3, 1)
-            at_x(copy_x, i + 3, 1)
-            at(quantise_v, i)
-            at(regroup_vector, i + 2)
-            at(finish, i - 1, 3)
-            at(multiply, i, 0)
-            at(multiply, i, 1)
-            at(transpose_v, i + 1, 0)
-            at(transpose_v, i + 1, 1)
-            at(copy_v, i + 1, 0)
-            at(copy_v, i + 1, 1)
+        for i in range(-3, B + 1):
             at_x(quantise_x, i + 2)
+            at(quantise_v, i)
             at(quantise_att, i + 1)
             at(regroup_gpsimd, i + 3)
+            at(regroup_vector, i + 2)
+            at(finish, i - 1, 3)
+            at(add_bias, i + 1, 2)
+            at(add_bias, i + 1, 3)
+            at(project, i + 2, 0)
+            at(project, i + 2, 1)
+            at(multiply, i, 0)
+            at(multiply, i, 1)
+            at(copy_v, i + 1, 0)
+            at(transpose_v, i + 1, 1)
+            at(multiply, i, 2)
+            at_x(copy_x, i + 3, 0)
+            at_x(transpose_x, i + 4, 0)
+            at_x(copy_x, i + 3, 1)
+            at(add_bias, i + 2, 0)
+            at(add_bias, i + 2, 1)
+            at(project, i + 2, 2)
+            at(project, i + 2, 3)
+            at_x(transpose_x, i + 4, 1)
+            at(copy_v, i + 1, 1)
+            at(transpose_v, i + 2, 0)
             at(finish, i, 0)
+            at(multiply, i, 3)
             at(finish, i, 1)
+            at(finish, i, 2)

@@ -22,7 +22,7 @@ BANKS = {"x": 2, "v": 2, "vt": 1, "o": 3}
 WARM_UPS = 4
 VECTOR_SAMPLES = 2
 GPSIMD_COLS = 384
-FINE_STORES = 3
+STORE_GROUPS = (4, 4, 4, 4, 2, 2, 1, 1)
 
 FLOPS = 2 * B * (N * N * N + N * N * N)
 
@@ -35,7 +35,7 @@ def tile_dualcrossmodalattention_pb_t_kernel(tc, x, Wv1, bv1, att2, gamma2, y, o
         inputs = ctx.enter_context(tc.tile_pool(name="inputs", bufs=B))
         work = ctx.enter_context(tc.tile_pool(name="work", bufs=3))
         quantised = ctx.enter_context(tc.tile_pool(name="quantised", bufs=3))
-        results = ctx.enter_context(tc.tile_pool(name="results", bufs=10))
+        results = ctx.enter_context(tc.tile_pool(name="results", bufs=5))
         psum = ctx.enter_context(tc.psum_pool(name="psum", bufs=1))
 
         def bank(kind, shape):
@@ -60,12 +60,12 @@ def tile_dualcrossmodalattention_pb_t_kernel(tc, x, Wv1, bv1, att2, gamma2, y, o
         nc.vector.memset(ones[:], 1.0)
         small = const.tile([P, GAMMA_COLS], BF16)
         nc.vector.memset(small[:], 0.0)
-        nc.sync.dma_start(out=small[0:1, 0:1], in_=gamma2.rearrange("(o g) -> o g", o=1))
+        nc.scalar.dma_start(out=small[0:1, 0:1], in_=gamma2.rearrange("(o g) -> o g", o=1))
         load_half(x_in[0], x[0], 0)
         load_half(x_in[0], x[0], 1)
         load_half(w_sb, Wv1, 1)
         bias_sb = const.tile([P, PACK], BF16)
-        nc.sync.dma_start(out=bias_sb[:], in_=bv1.rearrange("(p j) -> p j", j=PACK))
+        nc.scalar.dma_start(out=bias_sb[:], in_=bv1.rearrange("(p j) -> p j", j=PACK))
         for i in range(-4, B):
             if 1 <= i + 5 < B:
                 x_in[i + 5] = load_rows(x[i + 5], "x_sb")
@@ -199,26 +199,22 @@ def tile_dualcrossmodalattention_pb_t_kernel(tc, x, Wv1, bv1, att2, gamma2, y, o
             o_banks[b, c] = bank("o", [P, N])
             mx_pass(o_banks[b, c][:], v_mx[b], c, att_mx[b])
 
-        def store(b, first, end):
-            rows = out[b].rearrange("(p c) m -> p c m", c=PACK)[:, first:end, :]
-            pair = first // 2
-            nc.sync.dma_start(out=rows, in_=results_of[b, pair][:, first - 2 * pair : end - 2 * pair, :])
-
-        def result_rows(b, c):
-            if c % 2 == 0:
-                results_of[b, c // 2] = results.tile([P, 2, N], F32, tag="res", name="res")
-            return results_of[b, c // 2][:, c % 2, :]
-
         def finish(b, c):
-            res = result_rows(b, c)
-            y_rows = y_in[b][:, c * N : (c + 1) * N]
+            if c == 0:
+                results_of[b] = results.tile([P, PACK, N], F32, tag="res", name="res")
             nc.vector.scalar_tensor_tensor(
-                out=res, in0=o_banks[b, c][:], scalar=gamma_bc[:, 0:1], in1=y_rows, op0=MULT, op1=ADD
+                out=results_of[b][:, c, :],
+                in0=o_banks[b, c][:],
+                scalar=gamma_bc[:, 0:1],
+                in1=y_in[b][:, c * N : (c + 1) * N],
+                op0=MULT,
+                op1=ADD,
             )
-            if b >= B - FINE_STORES:
-                store(b, c, c + 1)
-            elif c % 2 == 1:
-                store(b, c - 1, c + 1)
+            groups = STORE_GROUPS[b]
+            if (c + 1) % groups == 0:
+                stored = slice(c + 1 - groups, c + 1)
+                rows = out[b].rearrange("(p c) m -> p c m", c=PACK)
+                nc.sync.dma_start(out=rows[:, stored, :], in_=results_of[b][:, stored, :])
 
         att_pool = ctx.enter_context(tc.tile_pool(name="att_pool", bufs=2))
         w_values = values_tile(const, "w_values")
@@ -228,15 +224,15 @@ def tile_dualcrossmodalattention_pb_t_kernel(tc, x, Wv1, bv1, att2, gamma2, y, o
         for h in range(2):
             transpose_x(0, h)
             copy_x(0, h)
-        gamma_ps = bank("vt", [P, GAMMA_COLS])
-        nc.tensor.matmul(out=gamma_ps[:], lhsT=ones[:], rhs=small[:], start=True, stop=True)
         x_mx[0] = quantised_tiles(quantised, "x")
         quantise_columns(x_mx[0], x_values[0], 0, N // 2)
-        gamma_bc = const.tile([P, 1], F32)
-        nc.vector.tensor_copy(out=gamma_bc[:], in_=gamma_ps[:, 0:1])
         quantise_columns(x_mx[0], x_values[0], N // 2, N)
         interleave_half(w_values, transpose_half(w_sb, 1, "o"), 1, nc.vector.tensor_copy)
         quantise_columns(w_mx, w_values, N // 2, N)
+        gamma_ps = bank("o", [P, GAMMA_COLS])
+        nc.tensor.matmul(out=gamma_ps[:], lhsT=ones[:], rhs=small[:], start=True, stop=True)
+        gamma_bc = const.tile([P, 1], F32)
+        nc.vector.tensor_copy(out=gamma_bc[:], in_=gamma_ps[:, 0:1])
 
         def at(stage, b, *which):
             if 0 <= b < B:

from contextlib import ExitStack

import concourse.mybir as mybir
from concourse.masks import make_identity

BF16 = mybir.dt.bfloat16
F32 = mybir.dt.float32
U32 = mybir.dt.uint32
U8 = mybir.dt.uint8
FP8X4 = mybir.dt.float8_e4m3fn_x4
ADD = mybir.AluOpType.add
MULT = mybir.AluOpType.mult
IDENTITY = mybir.ActivationFunctionType.Identity

B = 8
N = 512
P = 128
PACK = 4
PAIR = 2
GAMMA_COLS = 64
BANKS = {"x": 2, "v": 2, "vt": 1, "o": 3}
WARM_UPS = 4
VECTOR_SAMPLES = 2
GPSIMD_COLS = 384
STORE_GROUPS = (4, 4, 4, 4, 2, 2, 1, 1)

FLOPS = 2 * B * (N * N * N + N * N * N)


def tile_dualcrossmodalattention_pb_t_kernel(tc, x, Wv1, bv1, att2, gamma2, y, out):
    nc = tc.nc
    with ExitStack() as ctx:
        ctx.enter_context(tc.manual_schedule())
        const = ctx.enter_context(tc.tile_pool(name="const", bufs=1))
        inputs = ctx.enter_context(tc.tile_pool(name="inputs", bufs=B))
        work = ctx.enter_context(tc.tile_pool(name="work", bufs=3))
        quantised = ctx.enter_context(tc.tile_pool(name="quantised", bufs=3))
        results = ctx.enter_context(tc.tile_pool(name="results", bufs=5))
        psum = ctx.enter_context(tc.psum_pool(name="psum", bufs=1))

        def bank(kind, shape):
            return psum.tile(shape, F32, tag=kind, name=kind + "_ps", bufs=BANKS[kind])

        def load_rows(matrix, name):
            rows_sb = inputs.tile([P, PACK * N], BF16, tag=name, name=name)
            nc.sync.dma_start(out=rows_sb[:], in_=matrix.rearrange("(p j) c -> p (j c)", j=PACK))
            return rows_sb

        def load_half(rows_sb, matrix, h):
            nc.sync.dma_start(
                out=rows_sb[:, h * 2 * N : (h + 1) * 2 * N],
                in_=matrix.rearrange("(p h j) c -> p h (j c)", h=2, j=2)[:, h, :],
            )

        x_in, att_in, y_in = {}, {}, {}
        w_sb = const.tile([P, PACK * N], BF16)
        x_in[0] = inputs.tile([P, PACK * N], BF16, tag="x_sb", name="x_sb")
        load_half(w_sb, Wv1, 0)
        ones = const.tile([P, P], BF16)
        nc.vector.memset(ones[:], 1.0)
        small = const.tile([P, GAMMA_COLS], BF16)
        nc.vector.memset(small[:], 0.0)
        nc.scalar.dma_start(out=small[0:1, 0:1], in_=gamma2.rearrange("(o g) -> o g", o=1))
        load_half(x_in[0], x[0], 0)
        load_half(x_in[0], x[0], 1)
        load_half(w_sb, Wv1, 1)
        bias_sb = const.tile([P, PACK], BF16)
        nc.scalar.dma_start(out=bias_sb[:], in_=bv1.rearrange("(p j) -> p j", j=PACK))
        for i in range(-4, B):
            if 1 <= i + 5 < B:
                x_in[i + 5] = load_rows(x[i + 5], "x_sb")
            if 0 <= i + 4 < B:
                att_in[i + 4] = load_rows(att2[i + 4], "att_sb")
            if 0 <= i + 2 < B:
                y_in[i + 2] = load_rows(y[i + 2], "y_sb")

        ident = const.tile([P, P], F32)
        make_identity(nc, ident[:])
        idle_ps = bank("o", [P, N])
        for k in range(WARM_UPS):
            nc.tensor.matmul(
                out=idle_ps[:], lhsT=ones[:], rhs=ones[:, 0:1].to_broadcast([P, N]), start=True, stop=True
            )

        def values_tile(pool, name):
            return pool.tile([P, PACK * N], BF16, tag=name, name=name, align_bytes=64)

        def quantised_tiles(pool, name):
            codes = pool.tile([P, N], U32, tag=name + "_codes", name=name + "_codes", align_bytes=64)
            scales = pool.tile([P, N], U8, tag=name + "_scales", name=name + "_scales", align_bytes=64)
            return codes, scales

        def quantise_columns(operand, values, first, end):
            nc.vector.quantize_mx(
                out=operand[0][:, first:end].bitcast(FP8X4),
                scales=operand[1][:, first:end],
                in_=values[:, PACK * first : PACK * end],
            )

        def quantise(name, values):
            operand = quantised_tiles(quantised, name)
            quantise_columns(operand, values, 0, N)
            return operand

        def mx_pass(acc, stationary, j, moving):
            cols = slice(j * P, (j + 1) * P)
            nc.tensor.matmul_mx(
                out=acc,
                lhsT=stationary[0][:, cols].bitcast(FP8X4),
                lhsT_scale=stationary[1][:, cols],
                rhs=moving[0][:].bitcast(FP8X4),
                rhs_scale=moving[1][:],
                start=True,
                stop=True,
            )

        def transpose_half(rows_sb, h, kind):
            words = rows_sb[:].bitcast(F32)
            flip = bank(kind, [P, PAIR, 2 * P])
            for jj in range(2):
                for u in range(PAIR):
                    first = (2 * h + jj) * (N // PAIR) + u * P
                    nc.tensor.transpose(
                        flip[:, u, jj * P : (jj + 1) * P], words[:, first : first + P], ident[:]
                    )
            return flip

        def interleave_half(values, flip, h, copy):
            value_words = values[:].bitcast(F32).rearrange("q (c u) -> q c u", u=PAIR)
            copy(
                out=value_words[:, h * 2 * P : (h + 1) * 2 * P, :],
                in_=flip[:].rearrange("q u c -> q c u"),
            )

        x_flips, x_values, v_rows, v_flips, v_values, att_values = {}, {}, {}, {}, {}, {}
        x_mx, att_mx, v_mx, v_banks, o_banks, results_of = {}, {}, {}, {}, {}, {}

        def transpose_x(b, h):
            x_flips[b, h] = transpose_half(x_in[b], h, "x")

        def copy_x(b, h):
            if h == 0:
                x_values[b] = values_tile(work, "x_values")
            copy = nc.vector.tensor_copy if (b, h) == (2, 1) else nc.scalar.copy
            interleave_half(x_values[b], x_flips[b, h], h, copy)

        def quantise_x(b):
            x_mx[b] = quantise("x", x_values[b])

        def project(b, j):
            v_banks[b, j] = bank("v", [P, N])
            mx_pass(v_banks[b, j][:], w_mx, j, x_mx[b])

        def add_bias(b, j):
            if j == 0:
                v_rows[b] = work.tile([P, PACK * N], BF16, tag="v_rows", name="v_rows")
            nc.scalar.activation(
                out=v_rows[b][:, j * N : (j + 1) * N].rearrange("p (u q e) -> p u q e", u=PAIR, e=PAIR),
                in_=v_banks[b, j][:].rearrange("p (u e q) -> p u q e", u=PAIR, e=PAIR),
                func=IDENTITY,
                bias=bias_sb[:, j : j + 1],
            )

        def transpose_v(b, h):
            v_flips[b, h] = transpose_half(v_rows[b], h, "vt")

        def copy_v(b, h):
            if h == 0:
                v_values[b] = values_tile(work, "v_values")
            interleave_half(v_values[b], v_flips[b, h], h, nc.scalar.copy)

        def quantise_v(b):
            v_mx[b] = quantise("v", v_values[b])

        def regroup_att(b, first, end, copy):
            if b not in att_values:
                att_values[b] = att_pool.tile(
                    [P, PACK * N], BF16, tag="att_values", name="att_values", align_bytes=64
                )
            copy(
                out=att_values[b][:].rearrange("p (c j) -> p c j", j=PACK)[:, first:end, :],
                in_=att_in[b][:].rearrange("p (j c) -> p c j", j=PACK)[:, first:end, :],
            )

        def gpsimd_copy(out, in_):
            nc.gpsimd.tensor_scalar(out=out, in0=in_, scalar1=1.0, scalar2=0.0, op0=MULT, op1=ADD)

        def regroup_gpsimd(b):
            if b >= VECTOR_SAMPLES:
                regroup_att(b, 0, GPSIMD_COLS, gpsimd_copy)

        def regroup_vector(b):
            regroup_att(b, GPSIMD_COLS if b >= VECTOR_SAMPLES else 0, N, nc.vector.tensor_copy)

        def quantise_att(b):
            att_mx[b] = quantise("att", att_values[b])

        def multiply(b, c):
            o_banks[b, c] = bank("o", [P, N])
            mx_pass(o_banks[b, c][:], v_mx[b], c, att_mx[b])

        def finish(b, c):
            if c == 0:
                results_of[b] = results.tile([P, PACK, N], F32, tag="res", name="res")
            nc.vector.scalar_tensor_tensor(
                out=results_of[b][:, c, :],
                in0=o_banks[b, c][:],
                scalar=gamma_bc[:, 0:1],
                in1=y_in[b][:, c * N : (c + 1) * N],
                op0=MULT,
                op1=ADD,
            )
            groups = STORE_GROUPS[b]
            if (c + 1) % groups == 0:
                stored = slice(c + 1 - groups, c + 1)
                rows = out[b].rearrange("(p c) m -> p c m", c=PACK)
                nc.sync.dma_start(out=rows[:, stored, :], in_=results_of[b][:, stored, :])

        att_pool = ctx.enter_context(tc.tile_pool(name="att_pool", bufs=2))
        w_values = values_tile(const, "w_values")
        w_mx = quantised_tiles(const, "w")
        interleave_half(w_values, transpose_half(w_sb, 0, "o"), 0, nc.vector.tensor_copy)
        quantise_columns(w_mx, w_values, 0, N // 2)
        for h in range(2):
            transpose_x(0, h)
            copy_x(0, h)
        x_mx[0] = quantised_tiles(quantised, "x")
        quantise_columns(x_mx[0], x_values[0], 0, N // 2)
        quantise_columns(x_mx[0], x_values[0], N // 2, N)
        interleave_half(w_values, transpose_half(w_sb, 1, "o"), 1, nc.vector.tensor_copy)
        quantise_columns(w_mx, w_values, N // 2, N)
        gamma_ps = bank("o", [P, GAMMA_COLS])
        nc.tensor.matmul(out=gamma_ps[:], lhsT=ones[:], rhs=small[:], start=True, stop=True)
        gamma_bc = const.tile([P, 1], F32)
        nc.vector.tensor_copy(out=gamma_bc[:], in_=gamma_ps[:, 0:1])

        def at(stage, b, *which):
            if 0 <= b < B:
                stage(b, *which)

        def at_x(stage, b, *which):
            if 1 <= b < B:
                stage(b, *which)

        for i in range(-3, B + 1):
            at_x(quantise_x, i + 2)
            at(quantise_v, i)
            at(quantise_att, i + 1)
            at(regroup_gpsimd, i + 3)
            at(regroup_vector, i + 2)
            at(finish, i - 1, 3)
            at(add_bias, i + 1, 2)
            at(add_bias, i + 1, 3)
            at(project, i + 2, 0)
            at(project, i + 2, 1)
            at(multiply, i, 0)
            at(multiply, i, 1)
            at(copy_v, i + 1, 0)
            at(transpose_v, i + 1, 1)
            at(multiply, i, 2)
            at_x(copy_x, i + 3, 0)
            at_x(transpose_x, i + 4, 0)
            at_x(copy_x, i + 3, 1)
            at(add_bias, i + 2, 0)
            at(add_bias, i + 2, 1)
            at(project, i + 2, 2)
            at(project, i + 2, 3)
            at_x(transpose_x, i + 4, 1)
            at(copy_v, i + 1, 1)
            at(transpose_v, i + 2, 0)
            at(finish, i, 0)
            at(multiply, i, 3)
            at(finish, i, 1)
            at(finish, i, 2)
